import numpy as np
import ml_dtypes


def mxq(x, axis, fmt="e4m3"):
    dtype, down = {"e4m3": (ml_dtypes.float8_e4m3fn, 7), "e5m2": (ml_dtypes.float8_e5m2, 14)}[fmt]
    v = np.moveaxis(np.asarray(x, np.float32).astype(ml_dtypes.bfloat16).astype(np.float64), axis, -1)
    blocks = v.reshape(v.shape[:-1] + (-1, 32))
    amax = np.abs(blocks).max(-1, keepdims=True)
    byte = np.maximum(np.where(amax > 0, np.frexp(amax)[1] - 1 + 127, 0) - down, 1)
    scale = np.exp2(byte - 127.0)
    codes = (blocks / scale).astype(np.float32).astype(dtype).astype(np.float64)
    return np.moveaxis((codes * scale).reshape(v.shape), -1, axis)


WIDE = False


def mx_kscale(k):
    if not WIDE:
        return np.ones(k)
    levels = np.array([18, -18])
    if k % 512:
        return np.exp2(np.random.permutation(np.resize(levels, k // 32))).repeat(32)
    a = np.empty((k // 512, 16))
    for p in range(k // 512):
        a[p, :8] = np.random.permutation(np.resize(levels, 8))
        for g in range(8):
            far = levels[np.abs(levels - a[p, g]) >= 10]
            a[p, g + 8] = far[np.random.randint(len(far))]
    return np.exp2(a.ravel()).repeat(32)


BF16 = ml_dtypes.bfloat16


def bf(x):
    return np.asarray(x, np.float32).astype(BF16)


def f64(x):
    return np.asarray(x).astype(np.float64)


N, D_H, D_OUT = 2048, 512, 512
THRESH = 1e-6
EPS = 1e-8
DEG, BG, DEAD, TINY = 16.0, 4.0, 0.125, 1e-15


def draw_mobility():
    u = np.random.random_sample((N, N))
    strong = np.random.random_sample((N, N)) < DEG / N
    dead = np.random.random_sample(N) < DEAD
    return u * (BG / N + strong) * np.where(dead, TINY, 1.0)[None, :]


def column_statistics(M):
    cs = M.sum(axis=0)
    A = M / (cs[None, :] + EPS)
    return cs, np.where(A > THRESH, A, 0.0).sum(axis=0)


def setup_inputs():
    u = mx_kscale(N)
    v = mx_kscale(D_OUT)
    s = mx_kscale(N)
    c = np.max(u) * np.max(s)
    h0 = bf(np.maximum(np.random.standard_normal((N, D_H)), 0.0))
    m0 = bf(draw_mobility())
    w0 = bf(np.random.standard_normal((D_H, D_OUT)) * 2.0 / np.sqrt(D_H))
    b_in = bf(np.random.standard_normal(D_OUT) * 0.2)
    g0 = 4.0 * np.random.standard_normal((N, D_OUT)) * np.exp2(np.random.randint(-6, 1, (N, 1)))
    cs, ws = column_statistics(f64(m0))
    row = np.where(ws > 0.0, u / c, 1.0 / s)
    return {'h1': bf(f64(h0) * s[:, None]),
            'mobility_matrix': bf(f64(m0) * c / u[None, :] / s[:, None]),
            'W_in': bf(f64(w0) / v[None, :]),
            'b_in': b_in,
            'col_sum': np.asarray(cs, np.float32),
            'w_sum': np.asarray(ws, np.float32),
            'grad_out': bf(g0 * row[:, None] * v[None, :])}


def reference(h1, mobility_matrix, W_in, b_in, col_sum, w_sum, grad_out):
    M = f64(mobility_matrix)
    cs = f64(col_sum)
    ws = f64(w_sum)
    g = f64(grad_out)
    has_edge = (ws > 0.0)[:, None]
    Mm = np.where(M > THRESH * (cs + EPS)[None, :], M, 0.0)
    dz2 = np.where(has_edge, g / ((ws + EPS) * (cs + EPS))[:, None], 0.0)
    dh = mxq(Mm, 1, 'e4m3') @ mxq(dz2, 0, 'e5m2')
    dz1 = dh + np.where(has_edge, 0.0, g)
    dx = mxq(dz1, 1, 'e5m2') @ mxq(f64(W_in), 1, 'e4m3').T
    dw = mxq(f64(h1), 0, 'e4m3').T @ mxq(dz1, 0, 'e5m2')
    return dx, dw

@@ -1,0 +1,510 @@
+from contextlib import ExitStack
+
+import concourse.mybir as mybir
+from concourse.masks import make_identity
+
+NODES, D = 2048, 512
+FLOPS = 2 * NODES * NODES * D + 2 * (2 * NODES * D * D)
+BYTES = 2 * (NODES * D + NODES * NODES + D * D + NODES * D) + 4 * 2 * NODES + 4 * (NODES * D + D * D)
+
+F32 = mybir.dt.float32
+BF16 = mybir.dt.bfloat16
+I32 = mybir.dt.int32
+U32 = mybir.dt.uint32
+U8 = mybir.dt.uint8
+E4M3 = mybir.dt.float8_e4m3fn_x4
+E5M2 = mybir.dt.float8_e5m2_x4
+ALU = mybir.AluOpType
+
+P = 128
+PACK = 4
+Q = NODES // (P * PACK)
+STEPS = 8
+R = 256
+
+
+def tile_mobilitygnn_pb_v_kernel(tc, h1, mobility_matrix, W_in, b_in, col_sum, w_sum, grad_out, out_0, out_1):
+    nc = tc.nc
+    vec, act, pe, gps, sync = nc.vector, nc.scalar, nc.tensor, nc.gpsimd, nc.sync
+
+    M_v = mobility_matrix.rearrange("(q p t) i -> q p t i", q=Q, p=P)
+    g_v = grad_out.rearrange("(q p t) d -> q p t d", q=Q, p=P)
+    h_v = h1.rearrange("(q p t) d -> q p t d", q=Q, p=P)
+    o_v = out_0.rearrange("(q p t) h -> q p t h", q=Q, p=P)
+    W_v = W_in.rearrange("(m p) d -> p m d", p=P)
+    cs_v = col_sum.rearrange("(q p t) -> p q t", q=Q, p=P)
+    ws_v = w_sum.rearrange("(q p t) -> p q t", q=Q, p=P)
+
+    with ExitStack() as ctx:
+        keep = ctx.enter_context(tc.tile_pool(name="keep", bufs=1))
+        work = ctx.enter_context(tc.tile_pool(name="work", bufs=2))
+        psum = ctx.enter_context(tc.psum_pool(name="psum", bufs=1))
+        ctx.enter_context(tc.manual_schedule())
+
+        def kt(name, shape, dtype):
+            return keep.tile(shape, dtype, name=name, tag=name, align_bytes=64)
+
+        def wt(name, shape, dtype, bufs):
+            return work.tile(shape, dtype, name=name, tag=name, bufs=bufs, align_bytes=64)
+
+        def bank(tag, shape):
+            return psum.tile(shape, F32, name=tag, tag=tag)
+
+        cs = kt("cs", [P, Q, PACK], F32)
+        ws = kt("ws", [P, Q, PACK], F32)
+        act.dma_start(out=cs[:], in_=cs_v)
+        act.dma_start(out=ws[:], in_=ws_v)
+        ident = kt("ident", [P, P], F32)
+        make_identity(nc, ident[:])
+
+        M0 = []
+        for g in range(Q):
+            piece = kt("M0_%d" % g, [P, 2, 512], BF16)
+            sync.dma_start(out=piece[:], in_=M_v[0][:, 0:2, 512 * g : 512 * (g + 1)])
+            M0.append(piece)
+        gsb = []
+        for q in range(Q):
+            t = kt("g_%d" % q, [P, PACK, D], BF16)
+            sync.dma_start(out=t[:], in_=g_v[q])
+            gsb.append(t)
+        Mk = {}
+
+        def load_M(k):
+            t = wt("M", [P, 2, NODES], BF16, 4)
+            sync.dma_start(out=t[:], in_=M_v[k // 2][:, 2 * (k % 2) : 2 * (k % 2) + 2, :])
+            Mk[k] = t
+
+        hsb = []
+
+        def load_h(q):
+            t = kt("h_%d" % q, [P, PACK, D], BF16)
+            sync.dma_start(out=t[:], in_=h_v[q])
+            hsb.append(t)
+
+        load_M(1)
+        wsb = kt("wsb", [P, PACK, D], BF16)
+        sync.dma_start(out=wsb[:], in_=W_v)
+        load_M(2)
+        load_h(0)
+        load_M(3)
+        load_h(1)
+        load_M(4)
+        load_h(2)
+        load_h(3)
+
+        thr = kt("thr", [P, Q, PACK], F32)
+        thr_i = kt("thr_i", [P, Q, PACK], I32)
+        thr_b = kt("thr_b", [P, Q, PACK], BF16)
+        wse = kt("wse", [P, Q, PACK], F32)
+        den = kt("den", [P, Q, PACK], F32)
+        rec = kt("rec", [P, Q, PACK], F32)
+        edge = kt("edge", [P, Q, PACK], F32)
+        fac = kt("fac", [P, Q, PACK], F32)
+        lone = kt("lone", [P, Q, PACK], F32)
+        vec.tensor_scalar(out=thr[:], in0=cs[:], scalar1=1e-8, scalar2=1e-6, op0=ALU.add, op1=ALU.mult)
+        vec.tensor_scalar(out=wse[:], in0=ws[:], scalar1=1e-8, scalar2=None, op0=ALU.add)
+        vec.tensor_scalar(out=thr_i[:], in0=thr[:].bitcast(I32), scalar1=-65536, scalar2=None, op0=ALU.bitwise_and)
+        vec.scalar_tensor_tensor(out=den[:], in0=cs[:], scalar=1e-8, in1=wse[:], op0=ALU.add, op1=ALU.mult)
+        vec.tensor_copy(out=thr_b[:], in_=thr_i[:].bitcast(F32))
+        vec.reciprocal(out=rec[:], in_=den[:])
+        vec.tensor_scalar(out=edge[:], in0=ws[:], scalar1=0.0, scalar2=None, op0=ALU.is_gt)
+        vec.tensor_scalar(out=lone[:], in0=ws[:], scalar1=0.0, scalar2=None, op0=ALU.is_le)
+        vec.tensor_tensor(out=fac[:], in0=rec[:], in1=edge[:], op=ALU.mult)
+
+        tr = {}
+        mask = {}
+        xm = {}
+        mcode, mscale = {}, {}
+
+        def T(k, g):
+            b = bank("tr%d" % g, [P, 2, R])
+            for tl in range(2):
+                if k == 0:
+                    words = M0[g][:, tl, :].bitcast(F32)
+                    off = 0
+                else:
+                    words = Mk[k][:, tl, :].bitcast(F32)
+                    off = 256 * g
+                for u in range(2):
+                    pe.transpose(b[:, u, P * tl : P * (tl + 1)], words[:, off + u : off + 256 : 2], ident[:])
+            tr[k, g] = b
+
+        def four(ap):
+            return ap.rearrange("p (u r e) -> p r u e", u=2, e=2)
+
+        def GT(k, g):
+            m = wt("mask", [P, R, PACK], BF16, 4)
+            src = four(tr[k, g][:].rearrange("p u r -> p (u r)").bitcast(BF16))
+            lim = thr_b[:, g, :].rearrange("p (u e) -> p u e", u=2).unsqueeze(1).to_broadcast([P, R, 2, 2])
+            vec.tensor_tensor(out=m[:].rearrange("p r (u e) -> p r u e", u=2), in0=src, in1=lim, op=ALU.is_gt)
+            mask[k, g] = m
+
+        def MUL(k, g):
+            x = wt("xm", [P, R, PACK], BF16, 4)
+            src = four(tr[k, g][:].rearrange("p u r -> p (u r)").bitcast(BF16))
+            vec.tensor_tensor(
+                out=x[:].rearrange("p r (u e) -> p r u e", u=2),
+                in0=src,
+                in1=mask[k, g][:].rearrange("p r (u e) -> p r u e", u=2),
+                op=ALU.mult,
+            )
+            xm[k, g] = x
+
+        def MQ(k, g):
+            if k not in mcode:
+                mcode[k] = wt("mcode", [P, Q, R], U32, 3)
+                mscale[k] = wt("mscale", [P, Q, R], U8, 3)
+            vec.quantize_mx(
+                out=mcode[k][:, g, :].bitcast(E4M3),
+                scales=mscale[k][:, g, :],
+                in_=xm[k, g][:].rearrange("p r j -> p (r j)"),
+            )
+
+        def quant(name, src, width, fmt):
+            code = kt(name + "_c", [P, width], U32)
+            scale = kt(name + "_s", [P, width], U8)
+            vec.quantize_mx(out=code[:].bitcast(fmt), scales=scale[:], in_=src[:].rearrange("p c j -> p (c j)"))
+            return code, scale
+
+        def interleave_act(dst, src, a, b):
+            act.copy(
+                out=dst[:, a:b, :].rearrange("p (c i) t -> p c t i", i=4),
+                in_=src[:, :, a:b].rearrange("p t (c i) -> p c t i", i=4),
+            )
+
+        def interleave_vec(dst, src, a, b):
+            vec.tensor_copy(
+                out=dst[:, a:b, :].rearrange("p (c i) t -> p c t i", i=4),
+                in_=src[:, :, a:b].rearrange("p t (c i) -> p c t i", i=4),
+            )
+
+        def interleave_gps(dst, src):
+            gps.tensor_scalar(
+                out=dst[:],
+                in0=src[:].rearrange("p t d -> p d t"),
+                scalar1=1.0, scalar2=0.0, op0=ALU.mult, op1=ALU.add,
+            )
+
+        zs, zi, z = {}, {}, {}
+
+        def DS(q):
+            t = wt("zs", [P, PACK, D], BF16, 2)
+            for j in range(PACK):
+                vec.tensor_scalar(out=t[:, j, :], in0=gsb[q][:, j, :], scalar1=fac[:, q, j : j + 1], scalar2=None, op0=ALU.mult)
+            zs[q] = t
+
+        def DI(q):
+            t = wt("zi", [P, D, PACK], BF16, 4)
+            if q % 2 == 0:
+                interleave_act(t, zs[q], 0, D)
+            else:
+                interleave_gps(t, zs[q])
+            zi[q] = t
+
+        def DQ(q):
+            z[q] = quant("z%d" % q, zi[q], D, E5M2)
+
+        dh = {}
+
+        def MM(k, tl, gs):
+            if gs[0] == 0:
+                dh[k, tl] = bank("dh%d" % tl, [P, D])
+            cols = slice(P * tl, P * (tl + 1))
+            for g in gs:
+                pe.matmul_mx(
+                    out=dh[k, tl][:],
+                    lhsT=mcode[k][:, g, cols].bitcast(E4M3),
+                    lhsT_scale=mscale[k][:, g, cols],
+                    rhs=z[g][0][:].bitcast(E5M2),
+                    rhs_scale=z[g][1][:],
+                    start=(g == 0),
+                    stop=(g == Q - 1),
+                )
+
+        dz1 = {}
+
+        def STT(k, tl):
+            q, t = k // 2, 2 * (k % 2) + tl
+            if t == 0:
+                dz1[q] = wt("dz1", [P, PACK, D], BF16, 2)
+            vec.scalar_tensor_tensor(
+                out=dz1[q][:, t, :], in0=gsb[q][:, t, :], scalar=lone[:, q, t : t + 1], in1=dh[k, tl][:],
+                op0=ALU.mult, op1=ALU.add,
+            )
+
+        xt, xg, dxc = {}, {}, {}
+
+        def X(k, tl):
+            q, t = k // 2, 2 * (k % 2) + tl
+            if tl == 0:
+                xt[k] = bank("xt", [P, 2, R])
+            words = dz1[q][:, t, :].bitcast(F32)
+            for u in range(2):
+                pe.transpose(xt[k][:, u, P * tl : P * (tl + 1)], words[:, u:256:2], ident[:])
+
+        def XC(k):
+            t = wt("xg", [P, R, PACK], BF16, 2)
+            act.copy(
+                out=t[:].rearrange("p r j -> p (r j)").bitcast(F32).rearrange("p (r u) -> p r u", u=2),
+                in_=xt[k][:].rearrange("p u r -> p r u"),
+            )
+            xg[k] = t
+
+        def XQ(k):
+            code = wt("dx_c", [P, R], U32, 3)
+            scale = wt("dx_s", [P, R], U8, 3)
+            vec.quantize_mx(out=code[:].bitcast(E5M2), scales=scale[:], in_=xg[k][:].rearrange("p r j -> p (r j)"))
+            dxc[k] = (code, scale)
+
+        ob, ops = {}, {}
+
+        def O(k, tl, tag):
+            b = bank(tag, [P, D])
+            cols = slice(P * tl, P * (tl + 1))
+            pe.matmul_mx(
+                out=b[:], lhsT=dxc[k][0][:, cols].bitcast(E5M2), lhsT_scale=dxc[k][1][:, cols],
+                rhs=wq[0][:].bitcast(E4M3), rhs_scale=wq[1][:], start=True, stop=True,
+            )
+            ops[k, tl] = b
+
+        def OE(k, tl, eng):
+            if tl == 0:
+                ob[k] = wt("ob", [P, 2, D], F32, 3)
+            if eng == "act":
+                act.copy(out=ob[k][:, tl, :], in_=ops[k, tl][:])
+            else:
+                vec.tensor_copy(out=ob[k][:, tl, :], in_=ops[k, tl][:])
+
+        def OS(k):
+            h = 2 * (k % 2)
+            sync.dma_start(out=o_v[k // 2][:, h : h + 2, :], in_=ob[k][:])
+
+        di, dq, hq, hi = {}, {}, {}, {}
+
+        def new_di(q):
+            di[q] = wt("di", [P, D, PACK], BF16, 2)
+
+        def IQ(q):
+            dq[q] = quant("d%d" % q, di[q], D, E5M2)
+
+        def HI(q):
+            t = wt("hi", [P, D, PACK], BF16, 2)
+            interleave_act(t, hsb[q], 0, D)
+            hi[q] = t
+
+        def HQ(q):
+            hq[q] = quant("h%dq" % q, hi[q], D, E4M3)
+
+        oc = {}
+
+        def OUT1(c, q):
+            if q == 0:
+                oc[c] = bank("tr%d" % c, [P, D])
+            cols = slice(P * c, P * (c + 1))
+            pe.matmul_mx(
+                out=oc[c][:], lhsT=hq[q][0][:, cols].bitcast(E4M3), lhsT_scale=hq[q][1][:, cols],
+                rhs=dq[q][0][:].bitcast(E5M2), rhs_scale=dq[q][1][:], start=(q == 0), stop=(q == Q - 1),
+            )
+
+        for g in range(Q):
+            T(0, g)
+        wg = kt("wg", [P, D, PACK], BF16)
+        wb = []
+
+        def WT(b):
+            t = bank("xt" if b == 0 else "o", [P, 2, R])
+            for m in range(2):
+                words = wsb[:, 2 * b + m, :].bitcast(F32)
+                for u in range(2):
+                    pe.transpose(t[:, u, P * m : P * (m + 1)], words[:, u:256:2], ident[:])
+            wb.append(t)
+
+        def WC(b):
+            act.copy(
+                out=wg[:, R * b : R * (b + 1), :].rearrange("p r j -> p (r j)").bitcast(F32).rearrange("p (r u) -> p r u", u=2),
+                in_=wb[b][:].rearrange("p u r -> p r u"),
+            )
+
+        def half(k, g0):
+            GT(k, g0)
+            GT(k, g0 + 1)
+            MUL(k, g0)
+            MUL(k, g0 + 1)
+
+        half(0, 0)
+        T(1, 0)
+        T(1, 1)
+        DS(0)
+        DI(0)
+        MQ(0, 0)
+        MQ(0, 1)
+        DS(1)
+        DI(1)
+        half(0, 2)
+        T(1, 2)
+        T(1, 3)
+        MQ(0, 2)
+        MQ(0, 3)
+        load_M(5)
+        half(1, 0)
+        WT(0)
+        WT(1)
+        DS(2)
+        DI(2)
+        WC(0)
+        T(2, 0)
+        T(2, 1)
+        MQ(1, 0)
+        MQ(1, 1)
+        DS(3)
+        DI(3)
+        WC(1)
+        DQ(0)
+        DQ(1)
+        half(1, 2)
+        T(2, 2)
+        T(2, 3)
+        MQ(1, 2)
+        MQ(1, 3)
+        DQ(2)
+        DQ(3)
+        wq = quant("w", wg, D, E4M3)
+        load_M(6)
+
+        def chain_mm(k):
+            for tl in range(2):
+                MM(k, tl, range(Q))
+
+        chain_mm(0)
+        half(2, 0)
+        T(3, 0)
+        T(3, 1)
+        MQ(2, 0)
+        MQ(2, 1)
+        STT(0, 0)
+        STT(0, 1)
+        X(0, 0)
+        X(0, 1)
+        XC(0)
+        chain_mm(1)
+        HI(0)
+        half(2, 2)
+        T(3, 2)
+        T(3, 3)
+        MQ(2, 2)
+        MQ(2, 3)
+        XQ(0)
+        load_M(7)
+        for k in range(3, STEPS):
+            if k == 4:
+                XQ(2)
+                O(1, 0, "o")
+                MM(3, 0, range(Q))
+                OE(1, 0, "act")
+                O(1, 1, "o")
+                MM(3, 1, range(Q))
+                OE(1, 1, "act")
+                OS(1)
+            elif k == 3:
+                O(0, 0, "o")
+                OE(0, 0, "act")
+                STT(1, 0)
+                STT(1, 1)
+                O(0, 1, "o")
+                OE(0, 1, "act")
+                OS(0)
+                X(1, 0)
+                X(1, 1)
+                XC(1)
+                chain_mm(2)
+            else:
+                XQ(k - 2)
+                O(k - 2, 0, "o")
+                MM(k - 1, 0, range(Q))
+                OE(k - 2, 0, "act")
+                O(k - 2, 1, "o")
+                MM(k - 1, 1, range(Q))
+                OE(k - 2, 1, "act")
+                OS(k - 2)
+            half(k, 0)
+            if k == 4:
+                O(2, 0, "o")
+                OE(2, 0, "act")
+                O(2, 1, "o")
+                OE(2, 1, "act")
+                OS(2)
+            if k + 1 < STEPS:
+                T(k + 1, 0)
+                T(k + 1, 1)
+            if k >= 4:
+                HQ(k - 4)
+            MQ(k, 0)
+            MQ(k, 1)
+            STT(k - 1, 0)
+            STT(k - 1, 1)
+            X(k - 1, 0)
+            X(k - 1, 1)
+            XC(k - 1)
+            half(k, 2)
+            if k == 3:
+                XQ(1)
+            if k == 5:
+                IQ(0)
+            if k == 7:
+                IQ(1)
+            if k + 1 < STEPS:
+                T(k + 1, 2)
+                T(k + 1, 3)
+            MQ(k, 2)
+            if k == STEPS - 1:
+                for tl in range(2):
+                    MM(k, tl, range(3))
+            MQ(k, 3)
+            if k % 2 == 0:
+                q = k // 2 - 1
+                if q == 1 or q == 2:
+                    new_di(q - 1)
+                    interleave_act(di[q - 1], dz1[q - 1], 0, D)
+            if k == 7:
+                new_di(2)
+                interleave_act(di[2], dz1[2], 0, D)
+            if k in (3, 4, 5):
+                HI(k - 2)
+        XQ(6)
+        MM(7, 0, [3])
+        MM(7, 1, [3])
+        STT(7, 0)
+        STT(7, 1)
+        IQ(2)
+        for c in range(4):
+            OUT1(c, 0)
+        X(7, 0)
+        X(7, 1)
+        XC(7)
+        O(6, 0, "o")
+        OE(6, 0, "act")
+        for c in range(4):
+            OUT1(c, 1)
+        new_di(3)
+        interleave_vec(di[3], dz1[3], 0, 320)
+        interleave_act(di[3], dz1[3], 320, D)
+        XQ(7)
+        IQ(3)
+        O(6, 1, "o")
+        OE(6, 1, "act")
+        OS(6)
+        O(7, 0, "dh0")
+        O(7, 1, "dh1")
+        for c in range(4):
+            OUT1(c, 2)
+        OE(7, 0, "vec")
+        OE(7, 1, "act")
+        OS(7)
+        for c in range(4):
+            OUT1(c, 3)
+            t = kt("oc%d" % c, [P, D], F32)
+            if c % 2 == 0:
+                vec.tensor_copy(out=t[:], in_=oc[c][:])
+            else:
+                act.copy(out=t[:], in_=oc[c][:])
+            sync.dma_start(out=out_1[P * c : P * (c + 1), :], in_=t[:])

@@ -15,6 +15,7 @@ U8 = mybir.dt.uint8
 E4M3 = mybir.dt.float8_e4m3fn_x4
 E5M2 = mybir.dt.float8_e5m2_x4
 ALU = mybir.AluOpType
+ACTF = mybir.ActivationFunctionType
 
 P = 128
 PACK = 4
@@ -62,29 +63,30 @@ def tile_mobilitygnn_pb_v_kernel(tc, h1, mobility_matrix, W_in, b_in, col_sum, w
             piece = kt("M0_%d" % g, [P, 2, 512], BF16)
             sync.dma_start(out=piece[:], in_=M_v[0][:, 0:2, 512 * g : 512 * (g + 1)])
             M0.append(piece)
-        gsb = []
-        for q in range(Q):
-            t = kt("g_%d" % q, [P, PACK, D], BF16)
-            sync.dma_start(out=t[:], in_=g_v[q])
-            gsb.append(t)
+        gsb = {}
         Mk = {}
+        hsb = {}
+
+        def load_g(q):
+            gsb[q] = kt("g_%d" % q, [P, PACK, D], BF16)
+            sync.dma_start(out=gsb[q][:], in_=g_v[q])
 
         def load_M(k):
-            t = wt("M", [P, 2, NODES], BF16, 4)
-            sync.dma_start(out=t[:], in_=M_v[k // 2][:, 2 * (k % 2) : 2 * (k % 2) + 2, :])
-            Mk[k] = t
-
-        hsb = []
+            Mk[k] = wt("M", [P, 2, NODES], BF16, 4)
+            sync.dma_start(out=Mk[k][:], in_=M_v[k // 2][:, 2 * (k % 2) : 2 * (k % 2) + 2, :])
 
         def load_h(q):
-            t = kt("h_%d" % q, [P, PACK, D], BF16)
-            sync.dma_start(out=t[:], in_=h_v[q])
-            hsb.append(t)
+            hsb[q] = kt("h_%d" % q, [P, PACK, D], BF16)
+            sync.dma_start(out=hsb[q][:], in_=h_v[q])
 
+        load_g(0)
+        load_g(1)
         load_M(1)
+        load_g(2)
+        load_g(3)
+        load_M(2)
         wsb = kt("wsb", [P, PACK, D], BF16)
         sync.dma_start(out=wsb[:], in_=W_v)
-        load_M(2)
         load_h(0)
         load_M(3)
         load_h(1)
@@ -194,7 +196,7 @@ def tile_mobilitygnn_pb_v_kernel(tc, h1, mobility_matrix, W_in, b_in, col_sum, w
             zs[q] = t
 
         def DI(q):
-            t = wt("zi", [P, D, PACK], BF16, 4)
+            t = wt("zi", [P, D, PACK], BF16, 3)
             if q % 2 == 0:
                 interleave_act(t, zs[q], 0, D)
             else:
@@ -232,6 +234,25 @@ def tile_mobilitygnn_pb_v_kernel(tc, h1, mobility_matrix, W_in, b_in, col_sum, w
                 op0=ALU.mult, op1=ALU.add,
             )
 
+        dhs = {}
+
+        def MG(q, n):
+            for t in range(PACK):
+                if n == 1:
+                    vec.tensor_scalar(out=gsb[q][:, t, :], in0=gsb[q][:, t, :], scalar1=lone[:, q, t : t + 1], scalar2=None, op0=ALU.mult)
+                    continue
+                act.activation(out=gsb[q][:, t, :], in_=gsb[q][:, t, :], func=ACTF.Copy, scale=lone[:, q, t : t + 1])
+
+        def EV(k, tl):
+            dhs[k, tl] = wt("dhs", [P, D], F32, 3)
+            act.copy(out=dhs[k, tl][:], in_=dh[k, tl][:])
+
+        def ADD(k, tl):
+            q, t = k // 2, 2 * (k % 2) + tl
+            if t == 0:
+                dz1[q] = wt("dz1", [P, PACK, D], BF16, 2)
+            gps.tensor_tensor(out=dz1[q][:, t, :], in0=dhs[k, tl][:], in1=gsb[q][:, t, :], op=ALU.add)
+
         xt, xg, dxc = {}, {}, {}
 
         def X(k, tl):
@@ -242,13 +263,13 @@ def tile_mobilitygnn_pb_v_kernel(tc, h1, mobility_matrix, W_in, b_in, col_sum, w
             for u in range(2):
                 pe.transpose(xt[k][:, u, P * tl : P * (tl + 1)], words[:, u:256:2], ident[:])
 
-        def XC(k):
-            t = wt("xg", [P, R, PACK], BF16, 2)
+        def XC(k, a=0, b=R):
+            if a == 0:
+                xg[k] = wt("xg", [P, R, PACK], BF16, 2)
             act.copy(
-                out=t[:].rearrange("p r j -> p (r j)").bitcast(F32).rearrange("p (r u) -> p r u", u=2),
-                in_=xt[k][:].rearrange("p u r -> p r u"),
+                out=xg[k][:, a:b, :].rearrange("p r j -> p (r j)").bitcast(F32).rearrange("p (r u) -> p r u", u=2),
+                in_=xt[k][:, :, a:b].rearrange("p u r -> p r u"),
             )
-            xg[k] = t
 
         def XQ(k):
             code = wt("dx_c", [P, R], U32, 3)
@@ -281,16 +302,18 @@ def tile_mobilitygnn_pb_v_kernel(tc, h1, mobility_matrix, W_in, b_in, col_sum, w
 
         di, dq, hq, hi = {}, {}, {}, {}
 
-        def new_di(q):
-            di[q] = wt("di", [P, D, PACK], BF16, 2)
-
         def IQ(q):
             dq[q] = quant("d%d" % q, di[q], D, E5M2)
 
-        def HI(q):
-            t = wt("hi", [P, D, PACK], BF16, 2)
-            interleave_act(t, hsb[q], 0, D)
-            hi[q] = t
+        def HI(q, half_no):
+            if half_no == 0:
+                hi[q] = wt("hi", [P, D, PACK], BF16, 2)
+            interleave_act(hi[q], hsb[q], 256 * half_no, 256 * half_no + 256)
+
+        def DZI(q, half_no):
+            if half_no == 0:
+                di[q] = wt("di", [P, D, PACK], BF16, 2)
+            interleave_act(di[q], dz1[q], 256 * half_no, 256 * half_no + 256)
 
         def HQ(q):
             hq[q] = quant("h%dq" % q, hi[q], D, E4M3)
@@ -331,180 +354,145 @@ def tile_mobilitygnn_pb_v_kernel(tc, h1, mobility_matrix, W_in, b_in, col_sum, w
             MUL(k, g0)
             MUL(k, g0 + 1)
 
+        pieces = {
+            2: [(HI, 0, 0), (HI, 0, 1)],
+            3: [(DZI, 0, 0), (DZI, 0, 1), (MG, 3, 1)],
+            4: [(HI, 1, 0), (HI, 1, 1)],
+            5: [(DZI, 1, 0), (DZI, 1, 1), (HI, 2, 0)],
+            6: [(HI, 2, 1), (HI, 3, 0), (HI, 3, 1)],
+            7: [(DZI, 2, 0), (DZI, 2, 1)],
+        }
+        quants = {2: [], 3: [(HQ, 0)], 4: [(IQ, 0)], 5: [(HQ, 1)], 6: [(IQ, 1)], 7: [(HQ, 2), (HQ, 3)]}
+
         half(0, 0)
         T(1, 0)
         T(1, 1)
         DS(0)
         DI(0)
-        MQ(0, 0)
-        MQ(0, 1)
-        DS(1)
-        DI(1)
         half(0, 2)
         T(1, 2)
         T(1, 3)
-        MQ(0, 2)
-        MQ(0, 3)
+        DS(1)
+        DI(1)
+        for g in range(Q):
+            MQ(0, g)
         load_M(5)
-        half(1, 0)
-        WT(0)
-        WT(1)
         DS(2)
         DI(2)
-        WC(0)
-        T(2, 0)
-        T(2, 1)
-        MQ(1, 0)
-        MQ(1, 1)
         DS(3)
         DI(3)
-        WC(1)
+        MG(0, 0)
+        half(1, 0)
+        T(2, 0)
+        T(2, 1)
+        MG(1, 0)
+        MG(2, 0)
         DQ(0)
         DQ(1)
         half(1, 2)
         T(2, 2)
         T(2, 3)
-        MQ(1, 2)
-        MQ(1, 3)
+        WT(0)
+        WT(1)
+        WC(0)
+        WC(1)
         DQ(2)
         DQ(3)
+        MM(0, 0, range(Q))
+        EV(0, 0)
+        MM(0, 1, range(Q))
+        EV(0, 1)
+        for g in range(Q):
+            MQ(1, g)
         wq = quant("w", wg, D, E4M3)
+        ADD(0, 0)
+        ADD(0, 1)
         load_M(6)
 
-        def chain_mm(k):
-            for tl in range(2):
-                MM(k, tl, range(Q))
-
-        chain_mm(0)
-        half(2, 0)
-        T(3, 0)
-        T(3, 1)
-        MQ(2, 0)
-        MQ(2, 1)
-        STT(0, 0)
-        STT(0, 1)
-        X(0, 0)
-        X(0, 1)
-        XC(0)
-        chain_mm(1)
-        HI(0)
-        half(2, 2)
-        T(3, 2)
-        T(3, 3)
-        MQ(2, 2)
-        MQ(2, 3)
-        XQ(0)
-        load_M(7)
-        for k in range(3, STEPS):
-            if k == 4:
-                XQ(2)
-                O(1, 0, "o")
-                MM(3, 0, range(Q))
-                OE(1, 0, "act")
-                O(1, 1, "o")
-                MM(3, 1, range(Q))
-                OE(1, 1, "act")
-                OS(1)
-            elif k == 3:
-                O(0, 0, "o")
-                OE(0, 0, "act")
-                STT(1, 0)
-                STT(1, 1)
-                O(0, 1, "o")
-                OE(0, 1, "act")
-                OS(0)
-                X(1, 0)
-                X(1, 1)
-                XC(1)
-                chain_mm(2)
-            else:
-                XQ(k - 2)
-                O(k - 2, 0, "o")
-                MM(k - 1, 0, range(Q))
-                OE(k - 2, 0, "act")
-                O(k - 2, 1, "o")
-                MM(k - 1, 1, range(Q))
-                OE(k - 2, 1, "act")
-                OS(k - 2)
+        for k in range(2, STEPS):
+            last = k == STEPS - 1
+            if k > 2:
+                OE(k - 3, 0, "act")
+                OE(k - 3, 1, "act")
+                OS(k - 3)
+            MM(k - 1, 0, range(Q))
+            EV(k - 1, 0)
+            MM(k - 1, 1, range(Q))
+            EV(k - 1, 1)
+            if k == 2:
+                X(0, 0)
+                X(0, 1)
+                XC(0)
             half(k, 0)
-            if k == 4:
-                O(2, 0, "o")
-                OE(2, 0, "act")
-                O(2, 1, "o")
-                OE(2, 1, "act")
-                OS(2)
-            if k + 1 < STEPS:
+            for f, q, n in pieces[k]:
+                f(q, n)
+            ADD(k - 1, 0)
+            ADD(k - 1, 1)
+            if not last:
                 T(k + 1, 0)
                 T(k + 1, 1)
-            if k >= 4:
-                HQ(k - 4)
-            MQ(k, 0)
-            MQ(k, 1)
-            STT(k - 1, 0)
-            STT(k - 1, 1)
+            else:
+                for c in range(2):
+                    OUT1(c, 0)
+                    OUT1(c, 1)
+            half(k, 2)
+            if not last:
+                T(k + 1, 2)
+                T(k + 1, 3)
             X(k - 1, 0)
             X(k - 1, 1)
             XC(k - 1)
-            half(k, 2)
-            if k == 3:
-                XQ(1)
-            if k == 5:
-                IQ(0)
-            if k == 7:
-                IQ(1)
-            if k + 1 < STEPS:
-                T(k + 1, 2)
-                T(k + 1, 3)
-            MQ(k, 2)
-            if k == STEPS - 1:
-                for tl in range(2):
-                    MM(k, tl, range(3))
-            MQ(k, 3)
-            if k % 2 == 0:
-                q = k // 2 - 1
-                if q == 1 or q == 2:
-                    new_di(q - 1)
-                    interleave_act(di[q - 1], dz1[q - 1], 0, D)
-            if k == 7:
-                new_di(2)
-                interleave_act(di[2], dz1[2], 0, D)
-            if k in (3, 4, 5):
-                HI(k - 2)
+            if last:
+                for c in range(2, 4):
+                    OUT1(c, 0)
+                    OUT1(c, 1)
+            XQ(k - 2)
+            O(k - 2, 0, "o")
+            O(k - 2, 1, "dh1")
+            for g in range(Q):
+                MQ(k, g)
+                if last:
+                    MM(k, 0, [g])
+                    MM(k, 1, [g])
+            for f, q in quants[k]:
+                f(q)
+            if k == 2:
+                load_M(7)
+        OE(5, 0, "act")
+        OE(5, 1, "act")
+        OS(5)
         XQ(6)
-        MM(7, 0, [3])
-        MM(7, 1, [3])
-        STT(7, 0)
-        STT(7, 1)
         IQ(2)
-        for c in range(4):
-            OUT1(c, 0)
-        X(7, 0)
-        X(7, 1)
-        XC(7)
         O(6, 0, "o")
         OE(6, 0, "act")
-        for c in range(4):
-            OUT1(c, 1)
-        new_di(3)
-        interleave_vec(di[3], dz1[3], 0, 320)
-        interleave_act(di[3], dz1[3], 320, D)
+        STT(7, 0)
+        for c in range(2):
+            OUT1(c, 2)
+        X(7, 0)
+        XC(7, 0, P)
+        STT(7, 1)
+        for c in range(2, 4):
+            OUT1(c, 2)
+        X(7, 1)
+        di[3] = wt("di", [P, D, PACK], BF16, 2)
+        interleave_vec(di[3], dz1[3], 0, 384)
+        interleave_act(di[3], dz1[3], 384, D)
+        XC(7, P, R)
+        O(6, 1, "dh0")
         XQ(7)
         IQ(3)
-        O(6, 1, "o")
         OE(6, 1, "act")
         OS(6)
-        O(7, 0, "dh0")
+        O(7, 0, "o")
         O(7, 1, "dh1")
-        for c in range(4):
-            OUT1(c, 2)
-        OE(7, 0, "vec")
-        OE(7, 1, "act")
+        OE(7, 0, "act")
+        OE(7, 1, "vec")
         OS(7)
         for c in range(4):
             OUT1(c, 3)
             t = kt("oc%d" % c, [P, D], F32)
             if c % 2 == 0:
-                vec.tensor_copy(out=t[:], in_=oc[c][:])
-            else:
                 act.copy(out=t[:], in_=oc[c][:])
+            else:
+                vec.tensor_copy(out=t[:], in_=oc[c][:])
             sync.dma_start(out=out_1[P * c : P * (c + 1), :], in_=t[:])

@@ -21,6 +21,14 @@ P = 128
 PACK = 4
 Q = NODES // (P * PACK)
 STEPS = 8
+BIG = 1024.0
+VSHARE = 416
+NS0, NS1 = 3, 7
+
+
+def GADD(k, tl):
+    return False
+
 R = 256
 
 
@@ -58,11 +66,6 @@ def tile_mobilitygnn_pb_v_kernel(tc, h1, mobility_matrix, W_in, b_in, col_sum, w
         ident = kt("ident", [P, P], F32)
         make_identity(nc, ident[:])
 
-        M0 = []
-        for g in range(Q):
-            piece = kt("M0_%d" % g, [P, 2, 512], BF16)
-            sync.dma_start(out=piece[:], in_=M_v[0][:, 0:2, 512 * g : 512 * (g + 1)])
-            M0.append(piece)
         gsb = {}
         Mk = {}
         hsb = {}
@@ -79,14 +82,24 @@ def tile_mobilitygnn_pb_v_kernel(tc, h1, mobility_matrix, W_in, b_in, col_sum, w
             hsb[q] = kt("h_%d" % q, [P, PACK, D], BF16)
             sync.dma_start(out=hsb[q][:], in_=h_v[q])
 
+        M0 = {}
+
+        def load_M0(g):
+            M0[g] = kt("M0_%d" % g, [P, 2, 512], BF16)
+            sync.dma_start(out=M0[g][:], in_=M_v[0][:, 0:2, 512 * g : 512 * (g + 1)])
+
+        load_M0(0)
+        load_M0(1)
         load_g(0)
         load_g(1)
+        load_M0(2)
+        load_M0(3)
         load_M(1)
         load_g(2)
         load_g(3)
-        load_M(2)
         wsb = kt("wsb", [P, PACK, D], BF16)
         sync.dma_start(out=wsb[:], in_=W_v)
+        load_M(2)
         load_h(0)
         load_M(3)
         load_h(1)
@@ -103,6 +116,7 @@ def tile_mobilitygnn_pb_v_kernel(tc, h1, mobility_matrix, W_in, b_in, col_sum, w
         edge = kt("edge", [P, Q, PACK], F32)
         fac = kt("fac", [P, Q, PACK], F32)
         lone = kt("lone", [P, Q, PACK], F32)
+        nb = kt("nb", [P, Q, PACK], F32)
         vec.tensor_scalar(out=thr[:], in0=cs[:], scalar1=1e-8, scalar2=1e-6, op0=ALU.add, op1=ALU.mult)
         vec.tensor_scalar(out=wse[:], in0=ws[:], scalar1=1e-8, scalar2=None, op0=ALU.add)
         vec.tensor_scalar(out=thr_i[:], in0=thr[:].bitcast(I32), scalar1=-65536, scalar2=None, op0=ALU.bitwise_and)
@@ -112,6 +126,7 @@ def tile_mobilitygnn_pb_v_kernel(tc, h1, mobility_matrix, W_in, b_in, col_sum, w
         vec.tensor_scalar(out=edge[:], in0=ws[:], scalar1=0.0, scalar2=None, op0=ALU.is_gt)
         vec.tensor_scalar(out=lone[:], in0=ws[:], scalar1=0.0, scalar2=None, op0=ALU.is_le)
         vec.tensor_tensor(out=fac[:], in0=rec[:], in1=edge[:], op=ALU.mult)
+        vec.tensor_scalar(out=nb[:], in0=thr_i[:].bitcast(F32), scalar1=-BIG, scalar2=None, op0=ALU.mult)
 
         tr = {}
         mask = {}
@@ -131,35 +146,46 @@ def tile_mobilitygnn_pb_v_kernel(tc, h1, mobility_matrix, W_in, b_in, col_sum, w
                     pe.transpose(b[:, u, P * tl : P * (tl + 1)], words[:, off + u : off + 256 : 2], ident[:])
             tr[k, g] = b
 
-        def four(ap):
-            return ap.rearrange("p (u r e) -> p r u e", u=2, e=2)
+        def halves(k, g, a, b):
+            words = tr[k, g][:].rearrange("p u r -> p (u r)").bitcast(BF16)
+            return words.rearrange("p (u r e) -> p u r e", u=2, e=2)[:, :, a:b, :].rearrange("p u r e -> p r u e")
 
-        def GT(k, g):
-            m = wt("mask", [P, R, PACK], BF16, 4)
-            src = four(tr[k, g][:].rearrange("p u r -> p (u r)").bitcast(BF16))
-            lim = thr_b[:, g, :].rearrange("p (u e) -> p u e", u=2).unsqueeze(1).to_broadcast([P, R, 2, 2])
-            vec.tensor_tensor(out=m[:].rearrange("p r (u e) -> p r u e", u=2), in0=src, in1=lim, op=ALU.is_gt)
-            mask[k, g] = m
-
-        def MUL(k, g):
-            x = wt("xm", [P, R, PACK], BF16, 4)
-            src = four(tr[k, g][:].rearrange("p u r -> p (u r)").bitcast(BF16))
+        def GT(k, g, a=0, b=R):
+            if a == 0:
+                mask[k, g] = wt("mask", [P, R, PACK], BF16, 4)
+            lim = thr_b[:, g, :].rearrange("p (u e) -> p u e", u=2).unsqueeze(1).to_broadcast([P, b - a, 2, 2])
             vec.tensor_tensor(
-                out=x[:].rearrange("p r (u e) -> p r u e", u=2),
-                in0=src,
-                in1=mask[k, g][:].rearrange("p r (u e) -> p r u e", u=2),
-                op=ALU.mult,
+                out=mask[k, g][:, a:b, :].rearrange("p r (u e) -> p r u e", u=2), in0=halves(k, g, a, b), in1=lim, op=ALU.is_gt,
             )
-            xm[k, g] = x
 
-        def MQ(k, g):
+        def LIM(k, g):
+            s = wt("slim", [P, 2, R, 2], BF16, 2)
+            src = tr[k, g][:].rearrange("p u r -> p (u r)").bitcast(BF16).rearrange("p (u r e) -> p u r e", u=2, e=2)
+            for u in range(2):
+                for e in range(2):
+                    j = 2 * u + e
+                    act.activation(out=s[:, u, :, e], in_=src[:, u, :, e], func=ACTF.Relu, scale=BIG, bias=nb[:, g, j : j + 1])
+            mask[k, g] = s
+
+        def MUL(k, g, a=0, b=R):
+            if a == 0:
+                xm[k, g] = wt("xm", [P, R, PACK], BF16, 4)
+            if (k, g) in S_BANKS:
+                m, op = mask[k, g][:].rearrange("p u r e -> p r u e"), ALU.min
+            else:
+                m, op = mask[k, g][:, a:b, :].rearrange("p r (u e) -> p r u e", u=2), ALU.mult
+            vec.tensor_tensor(
+                out=xm[k, g][:, a:b, :].rearrange("p r (u e) -> p r u e", u=2), in0=halves(k, g, a, b), in1=m, op=op,
+            )
+
+        def MQ(k, g, a=0, b=R):
             if k not in mcode:
                 mcode[k] = wt("mcode", [P, Q, R], U32, 3)
                 mscale[k] = wt("mscale", [P, Q, R], U8, 3)
             vec.quantize_mx(
-                out=mcode[k][:, g, :].bitcast(E4M3),
-                scales=mscale[k][:, g, :],
-                in_=xm[k, g][:].rearrange("p r j -> p (r j)"),
+                out=mcode[k][:, g, a:b].bitcast(E4M3),
+                scales=mscale[k][:, g, a:b],
+                in_=xm[k, g][:, a:b, :].rearrange("p r j -> p (r j)"),
             )
 
         def quant(name, src, width, fmt):
@@ -180,13 +206,6 @@ def tile_mobilitygnn_pb_v_kernel(tc, h1, mobility_matrix, W_in, b_in, col_sum, w
                 in_=src[:, :, a:b].rearrange("p t (c i) -> p c t i", i=4),
             )
 
-        def interleave_gps(dst, src):
-            gps.tensor_scalar(
-                out=dst[:],
-                in0=src[:].rearrange("p t d -> p d t"),
-                scalar1=1.0, scalar2=0.0, op0=ALU.mult, op1=ALU.add,
-            )
-
         zs, zi, z = {}, {}, {}
 
         def DS(q):
@@ -197,10 +216,7 @@ def tile_mobilitygnn_pb_v_kernel(tc, h1, mobility_matrix, W_in, b_in, col_sum, w
 
         def DI(q):
             t = wt("zi", [P, D, PACK], BF16, 3)
-            if q % 2 == 0:
-                interleave_act(t, zs[q], 0, D)
-            else:
-                interleave_gps(t, zs[q])
+            interleave_act(t, zs[q], 0, D)
             zi[q] = t
 
         def DQ(q):
@@ -236,8 +252,13 @@ def tile_mobilitygnn_pb_v_kernel(tc, h1, mobility_matrix, W_in, b_in, col_sum, w
 
         dhs = {}
 
+        def on_gps(k, tl):
+            return GADD(k, tl)
+
         def MG(q, n):
             for t in range(PACK):
+                if not on_gps(2 * q + t // 2, t % 2):
+                    continue
                 if n == 1:
                     vec.tensor_scalar(out=gsb[q][:, t, :], in0=gsb[q][:, t, :], scalar1=lone[:, q, t : t + 1], scalar2=None, op0=ALU.mult)
                     continue
@@ -247,8 +268,15 @@ def tile_mobilitygnn_pb_v_kernel(tc, h1, mobility_matrix, W_in, b_in, col_sum, w
             dhs[k, tl] = wt("dhs", [P, D], F32, 3)
             act.copy(out=dhs[k, tl][:], in_=dh[k, tl][:])
 
+        def EVX(k, tl):
+            if on_gps(k, tl):
+                EV(k, tl)
+
         def ADD(k, tl):
             q, t = k // 2, 2 * (k % 2) + tl
+            if not on_gps(k, tl):
+                STT(k, tl)
+                return
             if t == 0:
                 dz1[q] = wt("dz1", [P, PACK, D], BF16, 2)
             gps.tensor_tensor(out=dz1[q][:, t, :], in0=dhs[k, tl][:], in1=gsb[q][:, t, :], op=ALU.add)
@@ -271,11 +299,11 @@ def tile_mobilitygnn_pb_v_kernel(tc, h1, mobility_matrix, W_in, b_in, col_sum, w
                 in_=xt[k][:, :, a:b].rearrange("p u r -> p r u"),
             )
 
-        def XQ(k):
-            code = wt("dx_c", [P, R], U32, 3)
-            scale = wt("dx_s", [P, R], U8, 3)
-            vec.quantize_mx(out=code[:].bitcast(E5M2), scales=scale[:], in_=xg[k][:].rearrange("p r j -> p (r j)"))
-            dxc[k] = (code, scale)
+        def XQ(k, a=0, b=R):
+            if a == 0:
+                dxc[k] = (wt("dx_c", [P, R], U32, 4), wt("dx_s", [P, R], U8, 4))
+            code, scale = dxc[k]
+            vec.quantize_mx(out=code[:, a:b].bitcast(E5M2), scales=scale[:, a:b], in_=xg[k][:, a:b, :].rearrange("p r j -> p (r j)"))
 
         ob, ops = {}, {}
 
@@ -329,8 +357,6 @@ def tile_mobilitygnn_pb_v_kernel(tc, h1, mobility_matrix, W_in, b_in, col_sum, w
                 rhs=dq[q][0][:].bitcast(E5M2), rhs_scale=dq[q][1][:], start=(q == 0), stop=(q == Q - 1),
             )
 
-        for g in range(Q):
-            T(0, g)
         wg = kt("wg", [P, D, PACK], BF16)
         wb = []
 
@@ -348,143 +374,207 @@ def tile_mobilitygnn_pb_v_kernel(tc, h1, mobility_matrix, W_in, b_in, col_sum, w
                 in_=wb[b][:].rearrange("p u r -> p r u"),
             )
 
+        S_BANKS = set([(k, 0) for k in range(NS0, NS1)] + [])
+
         def half(k, g0):
-            GT(k, g0)
-            GT(k, g0 + 1)
+            for g in (g0, g0 + 1):
+                if (k, g) not in S_BANKS:
+                    GT(k, g)
             MUL(k, g0)
             MUL(k, g0 + 1)
 
         pieces = {
-            2: [(HI, 0, 0), (HI, 0, 1)],
-            3: [(DZI, 0, 0), (DZI, 0, 1), (MG, 3, 1)],
-            4: [(HI, 1, 0), (HI, 1, 1)],
+            2: [(MG, 1, 0), (HI, 0, 0), (HI, 0, 1)],
+            3: [(DZI, 0, 0), (DZI, 0, 1), (MG, 2, 0)],
+            4: [(HI, 1, 0), (HI, 1, 1), (MG, 3, 0)],
             5: [(DZI, 1, 0), (DZI, 1, 1), (HI, 2, 0)],
             6: [(HI, 2, 1), (HI, 3, 0), (HI, 3, 1)],
-            7: [(DZI, 2, 0), (DZI, 2, 1)],
         }
-        quants = {2: [], 3: [(HQ, 0)], 4: [(IQ, 0)], 5: [(HQ, 1)], 6: [(IQ, 1)], 7: [(HQ, 2), (HQ, 3)]}
+        quants = {2: [], 3: [(HQ, 0)], 4: [(IQ, 0)], 5: [(HQ, 1)], 6: [(IQ, 1)]}
 
-        half(0, 0)
-        T(1, 0)
-        T(1, 1)
+        def run_pieces(k):
+            for f, q, n in pieces[k]:
+                if n is None:
+                    f(q)
+                else:
+                    f(q, n)
+
+        for g in range(Q):
+            T(0, g)
+        GT(0, 0)
+        GT(0, 1)
         DS(0)
         DI(0)
+        MUL(0, 0)
+        MUL(0, 1)
+        T(1, 0)
+        T(1, 1)
+        DS(1)
+        DI(1)
         half(0, 2)
         T(1, 2)
         T(1, 3)
-        DS(1)
-        DI(1)
         for g in range(Q):
             MQ(0, g)
         load_M(5)
         DS(2)
         DI(2)
+        half(1, 0)
         DS(3)
         DI(3)
         MG(0, 0)
-        half(1, 0)
+        WT(0)
+        WT(1)
+        WC(0)
+        WC(1)
         T(2, 0)
         T(2, 1)
-        MG(1, 0)
-        MG(2, 0)
+        for g in (0, 1):
+            if (2, g) in S_BANKS:
+                LIM(2, g)
         DQ(0)
         DQ(1)
         half(1, 2)
         T(2, 2)
         T(2, 3)
-        WT(0)
-        WT(1)
-        WC(0)
-        WC(1)
+        for g in (2, 3):
+            if (2, g) in S_BANKS:
+                LIM(2, g)
         DQ(2)
         DQ(3)
         MM(0, 0, range(Q))
-        EV(0, 0)
+        EVX(0, 0)
         MM(0, 1, range(Q))
-        EV(0, 1)
+        EVX(0, 1)
         for g in range(Q):
             MQ(1, g)
-        wq = quant("w", wg, D, E4M3)
-        ADD(0, 0)
-        ADD(0, 1)
         load_M(6)
-
-        for k in range(2, STEPS):
-            last = k == STEPS - 1
+        for k in range(2, STEPS - 1):
+            if k > 3:
+                OE(k - 4, 0, "act")
+                OE(k - 4, 1, "act")
+                OS(k - 4)
+            MM(k - 1, 0, [0, 1])
+            if k == 3:
+                XQ(0)
+                wq = quant("w", wg, D, E4M3)
             if k > 2:
-                OE(k - 3, 0, "act")
-                OE(k - 3, 1, "act")
-                OS(k - 3)
-            MM(k - 1, 0, range(Q))
-            EV(k - 1, 0)
-            MM(k - 1, 1, range(Q))
-            EV(k - 1, 1)
+                X(k - 2, 0)
+                X(k - 2, 1)
+                XC(k - 2)
+            MM(k - 1, 0, [2, 3])
+            EVX(k - 1, 0)
+            half(k, 0)
+            if k == 2:
+                ADD(0, 0)
+                ADD(0, 1)
+            ADD(k - 1, 0)
+            T(k + 1, 0)
+            if (k + 1, 0) in S_BANKS:
+                LIM(k + 1, 0)
+            if k != 2:
+                run_pieces(k)
+            MM(k - 1, 1, [0, 1])
+            T(k + 1, 1)
             if k == 2:
                 X(0, 0)
                 X(0, 1)
                 XC(0)
-            half(k, 0)
-            for f, q, n in pieces[k]:
-                f(q, n)
-            ADD(k - 1, 0)
-            ADD(k - 1, 1)
-            if not last:
-                T(k + 1, 0)
-                T(k + 1, 1)
-            else:
-                for c in range(2):
-                    OUT1(c, 0)
-                    OUT1(c, 1)
+            MM(k - 1, 1, [2, 3])
+            EVX(k - 1, 1)
             half(k, 2)
-            if not last:
-                T(k + 1, 2)
-                T(k + 1, 3)
-            X(k - 1, 0)
-            X(k - 1, 1)
-            XC(k - 1)
-            if last:
-                for c in range(2, 4):
-                    OUT1(c, 0)
-                    OUT1(c, 1)
-            XQ(k - 2)
-            O(k - 2, 0, "o")
-            O(k - 2, 1, "dh1")
-            for g in range(Q):
-                MQ(k, g)
-                if last:
-                    MM(k, 0, [g])
-                    MM(k, 1, [g])
+            T(k + 1, 2)
+            if k > 2:
+                O(k - 3, 0, "o")
+                O(k - 3, 1, "dh1" if not on_gps(k - 1, 1) else "dh1")
+            T(k + 1, 3)
+            if k == 2:
+                run_pieces(k)
+            if k > 2:
+                XQ(k - 2)
+            MQ(k, 0)
+            MQ(k, 1)
+            ADD(k - 1, 1)
+            MQ(k, 2)
+            MQ(k, 3)
             for f, q in quants[k]:
                 f(q)
             if k == 2:
                 load_M(7)
+        OE(3, 0, "act")
+        OE(3, 1, "act")
+        OS(3)
+        MM(6, 0, range(Q))
+        EVX(6, 0)
+        X(5, 0)
+        X(5, 1)
+        XC(5)
+        MM(6, 1, range(Q))
+        EVX(6, 1)
+        for g in range(Q):
+            GT(7, g, 0, P)
+        DZI(2, 0)
+        ADD(6, 0)
+        for g in range(Q):
+            MUL(7, g, 0, P)
+        DZI(2, 1)
+        O(4, 0, "o")
+        OE(4, 0, "act")
+        O(4, 1, "dh1")
+        OE(4, 1, "act")
+        OS(4)
+        for g in range(Q):
+            MQ(7, g, 0, P)
+        ADD(6, 1)
+        MM(7, 0, range(Q))
+        X(6, 0)
+        X(6, 1)
+        XC(6)
+        XQ(5)
+        HQ(2)
+        O(5, 0, "o")
         OE(5, 0, "act")
+        for g in range(Q):
+            GT(7, g, P, R)
+        STT(7, 0)
+        X(7, 0)
+        XC(7, 0, P)
+        O(5, 1, "o")
         OE(5, 1, "act")
         OS(5)
+        for g in range(Q):
+            MUL(7, g, P, R)
+        HQ(3)
         XQ(6)
+        OUT1(0, 0)
+        OUT1(0, 1)
+        OUT1(1, 0)
+        for g in range(Q):
+            MQ(7, g, P, R)
+            MM(7, 1, [g])
         IQ(2)
         O(6, 0, "o")
         OE(6, 0, "act")
-        STT(7, 0)
-        for c in range(2):
-            OUT1(c, 2)
-        X(7, 0)
-        XC(7, 0, P)
+        OUT1(1, 1)
         STT(7, 1)
-        for c in range(2, 4):
-            OUT1(c, 2)
         X(7, 1)
-        di[3] = wt("di", [P, D, PACK], BF16, 2)
-        interleave_vec(di[3], dz1[3], 0, 384)
-        interleave_act(di[3], dz1[3], 384, D)
         XC(7, P, R)
+        di[3] = wt("di", [P, D, PACK], BF16, 2)
+        interleave_vec(di[3], dz1[3], 0, VSHARE)
+        interleave_act(di[3], dz1[3], VSHARE, D)
         O(6, 1, "dh0")
-        XQ(7)
-        IQ(3)
         OE(6, 1, "act")
         OS(6)
+        for c, q in [(2, 0), (2, 1), (0, 2), (1, 2)]:
+            OUT1(c, q)
+        XQ(7, 0, P)
+        XQ(7, P, R)
         O(7, 0, "o")
+        OUT1(2, 2)
         O(7, 1, "dh1")
+        IQ(3)
+        for q in range(3):
+            OUT1(3, q)
         OE(7, 0, "act")
         OE(7, 1, "vec")
         OS(7)

@@ -100,12 +100,10 @@ def tile_mobilitygnn_pb_v_kernel(tc, h1, mobility_matrix, W_in, b_in, col_sum, w
         wsb = kt("wsb", [P, PACK, D], BF16)
         sync.dma_start(out=wsb[:], in_=W_v)
         load_M(2)
-        load_h(0)
         load_M(3)
-        load_h(1)
         load_M(4)
-        load_h(2)
-        load_h(3)
+        load_h(0)
+        load_h(1)
 
         thr = kt("thr", [P, Q, PACK], F32)
         thr_i = kt("thr_i", [P, Q, PACK], I32)
@@ -151,6 +149,8 @@ def tile_mobilitygnn_pb_v_kernel(tc, h1, mobility_matrix, W_in, b_in, col_sum, w
             return words.rearrange("p (u r e) -> p u r e", u=2, e=2)[:, :, a:b, :].rearrange("p u r e -> p r u e")
 
         def GT(k, g, a=0, b=R):
+            if (k, g) in S_BANKS:
+                return
             if a == 0:
                 mask[k, g] = wt("mask", [P, R, PACK], BF16, 4)
             lim = thr_b[:, g, :].rearrange("p (u e) -> p u e", u=2).unsqueeze(1).to_broadcast([P, b - a, 2, 2])
@@ -159,7 +159,7 @@ def tile_mobilitygnn_pb_v_kernel(tc, h1, mobility_matrix, W_in, b_in, col_sum, w
             )
 
         def LIM(k, g):
-            s = wt("slim", [P, 2, R, 2], BF16, 2)
+            s = wt("slim", [P, 2, R, 2], BF16, 4)
             src = tr[k, g][:].rearrange("p u r -> p (u r)").bitcast(BF16).rearrange("p (u r e) -> p u r e", u=2, e=2)
             for u in range(2):
                 for e in range(2):
@@ -171,7 +171,7 @@ def tile_mobilitygnn_pb_v_kernel(tc, h1, mobility_matrix, W_in, b_in, col_sum, w
             if a == 0:
                 xm[k, g] = wt("xm", [P, R, PACK], BF16, 4)
             if (k, g) in S_BANKS:
-                m, op = mask[k, g][:].rearrange("p u r e -> p r u e"), ALU.min
+                m, op = mask[k, g][:, :, a:b, :].rearrange("p u r e -> p r u e"), ALU.min
             else:
                 m, op = mask[k, g][:, a:b, :].rearrange("p r (u e) -> p r u e", u=2), ALU.mult
             vec.tensor_tensor(
@@ -200,6 +200,12 @@ def tile_mobilitygnn_pb_v_kernel(tc, h1, mobility_matrix, W_in, b_in, col_sum, w
                 in_=src[:, :, a:b].rearrange("p t (c i) -> p c t i", i=4),
             )
 
+        def interleave_gps(dst, src, a, b):
+            gps.tensor_scalar(
+                out=dst[:, a:b, :], in0=src[:, :, a:b].rearrange("p t d -> p d t"),
+                scalar1=1.0, scalar2=0.0, op0=ALU.mult, op1=ALU.add,
+            )
+
         def interleave_vec(dst, src, a, b):
             vec.tensor_copy(
                 out=dst[:, a:b, :].rearrange("p (c i) t -> p c t i", i=4),
@@ -216,8 +222,12 @@ def tile_mobilitygnn_pb_v_kernel(tc, h1, mobility_matrix, W_in, b_in, col_sum, w
 
         def DI(q):
             t = wt("zi", [P, D, PACK], BF16, 3)
-            interleave_act(t, zs[q], 0, D)
             zi[q] = t
+            if q % 2 == 0:
+                interleave_act(t, zs[q], 0, D)
+            else:
+                for a in range(0, D, 128):
+                    interleave_gps(t, zs[q], a, a + 128)
 
         def DQ(q):
             z[q] = quant("z%d" % q, zi[q], D, E5M2)
@@ -335,8 +345,9 @@ def tile_mobilitygnn_pb_v_kernel(tc, h1, mobility_matrix, W_in, b_in, col_sum, w
 
         def HI(q, half_no):
             if half_no == 0:
-                hi[q] = wt("hi", [P, D, PACK], BF16, 2)
-            interleave_act(hi[q], hsb[q], 256 * half_no, 256 * half_no + 256)
+                hi[q] = wt("hi", [P, D, PACK], BF16, 1)
+            for a in (256 * half_no, 256 * half_no + 128):
+                interleave_gps(hi[q], hsb[q], a, a + 128)
 
         def DZI(q, half_no):
             if half_no == 0:
@@ -374,7 +385,7 @@ def tile_mobilitygnn_pb_v_kernel(tc, h1, mobility_matrix, W_in, b_in, col_sum, w
                 in_=wb[b][:].rearrange("p u r -> p r u"),
             )
 
-        S_BANKS = set([(k, 0) for k in range(NS0, NS1)] + [])
+        S_BANKS = set([(k, 0) for k in range(NS0, NS1)] + [(1,1),(2,0),(2,1),(2,2),(3,2),(4,2),(5,2),(6,2),(7,0)])
 
         def half(k, g0):
             for g in (g0, g0 + 1):
@@ -384,13 +395,13 @@ def tile_mobilitygnn_pb_v_kernel(tc, h1, mobility_matrix, W_in, b_in, col_sum, w
             MUL(k, g0 + 1)
 
         pieces = {
-            2: [(MG, 1, 0), (HI, 0, 0), (HI, 0, 1)],
-            3: [(DZI, 0, 0), (DZI, 0, 1), (MG, 2, 0)],
-            4: [(HI, 1, 0), (HI, 1, 1), (MG, 3, 0)],
-            5: [(DZI, 1, 0), (DZI, 1, 1), (HI, 2, 0)],
-            6: [(HI, 2, 1), (HI, 3, 0), (HI, 3, 1)],
+            2: [(HI, 0, 0), (HI, 0, 1)],
+            3: [(HI, 1, 0), (HI, 1, 1), (DZI, 0, 0), (DZI, 0, 1)],
+            4: [(HI, 2, 0), (HI, 2, 1)],
+            5: [(HI, 3, 0), (HI, 3, 1), (DZI, 1, 0)],
+            6: [(DZI, 1, 1)],
         }
-        quants = {2: [], 3: [(HQ, 0)], 4: [(IQ, 0)], 5: [(HQ, 1)], 6: [(IQ, 1)]}
+        quants = {2: [(HQ, 0)], 3: [(HQ, 1)], 4: [(IQ, 0), (HQ, 2)], 5: [(HQ, 3)], 6: []}
 
         def run_pieces(k):
             for f, q, n in pieces[k]:
@@ -398,6 +409,11 @@ def tile_mobilitygnn_pb_v_kernel(tc, h1, mobility_matrix, W_in, b_in, col_sum, w
                     f(q)
                 else:
                     f(q, n)
+
+        def TL(k, g):
+            T(k, g)
+            if (k, g) in S_BANKS:
+                LIM(k, g)
 
         for g in range(Q):
             T(0, g)
@@ -407,45 +423,38 @@ def tile_mobilitygnn_pb_v_kernel(tc, h1, mobility_matrix, W_in, b_in, col_sum, w
         DI(0)
         MUL(0, 0)
         MUL(0, 1)
-        T(1, 0)
-        T(1, 1)
+        TL(1, 0)
+        TL(1, 1)
         DS(1)
         DI(1)
         half(0, 2)
-        T(1, 2)
-        T(1, 3)
+        TL(1, 2)
+        TL(1, 3)
         for g in range(Q):
             MQ(0, g)
         load_M(5)
+        load_h(2)
+        load_h(3)
         DS(2)
         DI(2)
         half(1, 0)
         DS(3)
         DI(3)
-        MG(0, 0)
         WT(0)
         WT(1)
         WC(0)
         WC(1)
-        T(2, 0)
-        T(2, 1)
-        for g in (0, 1):
-            if (2, g) in S_BANKS:
-                LIM(2, g)
+        TL(2, 0)
+        TL(2, 1)
         DQ(0)
         DQ(1)
         half(1, 2)
-        T(2, 2)
-        T(2, 3)
-        for g in (2, 3):
-            if (2, g) in S_BANKS:
-                LIM(2, g)
         DQ(2)
         DQ(3)
+        TL(2, 2)
+        TL(2, 3)
         MM(0, 0, range(Q))
-        EVX(0, 0)
         MM(0, 1, range(Q))
-        EVX(0, 1)
         for g in range(Q):
             MQ(1, g)
         load_M(6)
@@ -454,7 +463,7 @@ def tile_mobilitygnn_pb_v_kernel(tc, h1, mobility_matrix, W_in, b_in, col_sum, w
                 OE(k - 4, 0, "act")
                 OE(k - 4, 1, "act")
                 OS(k - 4)
-            MM(k - 1, 0, [0, 1])
+            MM(k - 1, 0, range(Q))
             if k == 3:
                 XQ(0)
                 wq = quant("w", wg, D, E4M3)
@@ -462,39 +471,30 @@ def tile_mobilitygnn_pb_v_kernel(tc, h1, mobility_matrix, W_in, b_in, col_sum, w
                 X(k - 2, 0)
                 X(k - 2, 1)
                 XC(k - 2)
-            MM(k - 1, 0, [2, 3])
-            EVX(k - 1, 0)
             half(k, 0)
             if k == 2:
-                ADD(0, 0)
-                ADD(0, 1)
-            ADD(k - 1, 0)
-            T(k + 1, 0)
-            if (k + 1, 0) in S_BANKS:
-                LIM(k + 1, 0)
-            if k != 2:
-                run_pieces(k)
-            MM(k - 1, 1, [0, 1])
-            T(k + 1, 1)
+                STT(0, 0)
+                STT(0, 1)
+            STT(k - 1, 0)
+            TL(k + 1, 0)
+            TL(k + 1, 1)
             if k == 2:
                 X(0, 0)
                 X(0, 1)
                 XC(0)
-            MM(k - 1, 1, [2, 3])
-            EVX(k - 1, 1)
+            run_pieces(k)
+            MM(k - 1, 1, range(Q))
             half(k, 2)
-            T(k + 1, 2)
+            TL(k + 1, 2)
+            TL(k + 1, 3)
             if k > 2:
                 O(k - 3, 0, "o")
-                O(k - 3, 1, "dh1" if not on_gps(k - 1, 1) else "dh1")
-            T(k + 1, 3)
-            if k == 2:
-                run_pieces(k)
+                O(k - 3, 1, "dh1")
             if k > 2:
                 XQ(k - 2)
             MQ(k, 0)
             MQ(k, 1)
-            ADD(k - 1, 1)
+            STT(k - 1, 1)
             MQ(k, 2)
             MQ(k, 3)
             for f, q in quants[k]:
@@ -531,50 +531,51 @@ def tile_mobilitygnn_pb_v_kernel(tc, h1, mobility_matrix, W_in, b_in, col_sum, w
         X(6, 1)
         XC(6)
         XQ(5)
-        HQ(2)
+        IQ(1)
         O(5, 0, "o")
+        O(5, 1, "dh1")
         OE(5, 0, "act")
+        OE(5, 1, "act")
+        OS(5)
         for g in range(Q):
             GT(7, g, P, R)
         STT(7, 0)
         X(7, 0)
         XC(7, 0, P)
-        O(5, 1, "o")
-        OE(5, 1, "act")
-        OS(5)
         for g in range(Q):
             MUL(7, g, P, R)
-        HQ(3)
         XQ(6)
-        OUT1(0, 0)
-        OUT1(0, 1)
-        OUT1(1, 0)
+        for c in range(2):
+            OUT1(c, 0)
+            OUT1(c, 1)
         for g in range(Q):
             MQ(7, g, P, R)
             MM(7, 1, [g])
         IQ(2)
-        O(6, 0, "o")
-        OE(6, 0, "act")
-        OUT1(1, 1)
+        XQ(7, 0, P)
+        OUT1(2, 0)
+        OUT1(2, 1)
         STT(7, 1)
         X(7, 1)
         XC(7, P, R)
         di[3] = wt("di", [P, D, PACK], BF16, 2)
         interleave_vec(di[3], dz1[3], 0, VSHARE)
         interleave_act(di[3], dz1[3], VSHARE, D)
+        O(6, 0, "o")
         O(6, 1, "dh0")
+        OE(6, 0, "act")
         OE(6, 1, "act")
         OS(6)
-        for c, q in [(2, 0), (2, 1), (0, 2), (1, 2)]:
-            OUT1(c, q)
-        XQ(7, 0, P)
+        OUT1(3, 0)
+        OUT1(3, 1)
+        O(7, 0, "dh1")
+        OUT1(0, 2)
+        OUT1(1, 2)
         XQ(7, P, R)
-        O(7, 0, "o")
         OUT1(2, 2)
-        O(7, 1, "dh1")
+        O(7, 1, "xt")
+        OUT1(3, 2)
         IQ(3)
-        for q in range(3):
-            OUT1(3, q)
         OE(7, 0, "act")
         OE(7, 1, "vec")
         OS(7)

@@ -5,7 +5,7 @@ from concourse.masks import make_identity
 
 NODES, D = 2048, 512
 FLOPS = 2 * NODES * NODES * D + 2 * (2 * NODES * D * D)
-BYTES = 2 * (NODES * D + NODES * NODES + D * D + NODES * D) + 4 * 2 * NODES + 4 * (NODES * D + D * D)
+BYTES = 2 * (NODES * NODES + 2 * NODES * D + D * D) + 4 * 2 * NODES + 4 * (NODES * D + D * D)
 
 F32 = mybir.dt.float32
 BF16 = mybir.dt.bfloat16
@@ -15,575 +15,514 @@ U8 = mybir.dt.uint8
 E4M3 = mybir.dt.float8_e4m3fn_x4
 E5M2 = mybir.dt.float8_e5m2_x4
 ALU = mybir.AluOpType
-ACTF = mybir.ActivationFunctionType
+ACT = mybir.ActivationFunctionType
 
 P = 128
 PACK = 4
-Q = NODES // (P * PACK)
-STEPS = 8
-BIG = 1024.0
-VSHARE = 416
-NS0, NS1 = 3, 7
+PASS = P * PACK
+PASSES = NODES // PASS
+ROWS = 2 * P
+STEPS = NODES // ROWS
+LAST = STEPS - 1
 
+THRESHOLD, EPS = 1e-6, 1e-8
+STEEP = 1024.0
 
-def GADD(k, tl):
-    return False
-
-R = 256
+CUT_ON_SCALAR = {0: (), 1: (1,), 2: (0, 1, 2), 3: (0, 2), 4: (0, 2), 5: (0, 2), 6: (0, 2), 7: (0, 1)}
+VECTOR_COLUMNS = 416
 
 
 def tile_mobilitygnn_pb_v_kernel(tc, h1, mobility_matrix, W_in, b_in, col_sum, w_sum, grad_out, out_0, out_1):
     nc = tc.nc
-    vec, act, pe, gps, sync = nc.vector, nc.scalar, nc.tensor, nc.gpsimd, nc.sync
+    pe, vec, act, gps, sync = nc.tensor, nc.vector, nc.scalar, nc.gpsimd, nc.sync
 
-    M_v = mobility_matrix.rearrange("(q p t) i -> q p t i", q=Q, p=P)
-    g_v = grad_out.rearrange("(q p t) d -> q p t d", q=Q, p=P)
-    h_v = h1.rearrange("(q p t) d -> q p t d", q=Q, p=P)
-    o_v = out_0.rearrange("(q p t) h -> q p t h", q=Q, p=P)
-    W_v = W_in.rearrange("(m p) d -> p m d", p=P)
-    cs_v = col_sum.rearrange("(q p t) -> p q t", q=Q, p=P)
-    ws_v = w_sum.rearrange("(q p t) -> p q t", q=Q, p=P)
+    m_rows = mobility_matrix.rearrange("(g p t) i -> g p t i", g=PASSES, p=P)
+    g_rows = grad_out.rearrange("(g p t) d -> g p t d", g=PASSES, p=P)
+    h_rows = h1.rearrange("(g p t) h -> g p t h", g=PASSES, p=P)
+    w_rows = W_in.rearrange("(m p) d -> p m d", p=P)
+    o_rows = out_0.rearrange("(g p t) h -> g p t h", g=PASSES, p=P)
+    col_sums = col_sum.rearrange("(g p t) -> p g t", g=PASSES, p=P)
+    w_sums = w_sum.rearrange("(g p t) -> p g t", g=PASSES, p=P)
 
     with ExitStack() as ctx:
         keep = ctx.enter_context(tc.tile_pool(name="keep", bufs=1))
-        work = ctx.enter_context(tc.tile_pool(name="work", bufs=2))
+        stream = ctx.enter_context(tc.tile_pool(name="stream", bufs=2))
         psum = ctx.enter_context(tc.psum_pool(name="psum", bufs=1))
         ctx.enter_context(tc.manual_schedule())
 
-        def kt(name, shape, dtype):
+        def kept(name, shape, dtype):
             return keep.tile(shape, dtype, name=name, tag=name, align_bytes=64)
 
-        def wt(name, shape, dtype, bufs):
-            return work.tile(shape, dtype, name=name, tag=name, bufs=bufs, align_bytes=64)
+        def streamed(name, shape, dtype, bufs):
+            return stream.tile(shape, dtype, name=name, tag=name, bufs=bufs, align_bytes=64)
 
-        def bank(tag, shape):
-            return psum.tile(shape, F32, name=tag, tag=tag)
+        def bank(name, shape):
+            return psum.tile(shape, F32, name=name, tag=name)
 
-        cs = kt("cs", [P, Q, PACK], F32)
-        ws = kt("ws", [P, Q, PACK], F32)
-        act.dma_start(out=cs[:], in_=cs_v)
-        act.dma_start(out=ws[:], in_=ws_v)
-        ident = kt("ident", [P, P], F32)
-        make_identity(nc, ident[:])
+        cs = kept("cs", [P, PASSES, PACK], F32)
+        ws = kept("ws", [P, PASSES, PACK], F32)
+        act.dma_start(out=cs[:], in_=col_sums)
+        act.dma_start(out=ws[:], in_=w_sums)
+        identity = kept("identity", [P, P], F32)
+        make_identity(nc, identity[:])
 
-        gsb = {}
-        Mk = {}
-        hsb = {}
+        first_m, m_sb, g_sb, h_sb = {}, {}, {}, {}
+
+        def load_first_m(g):
+            first_m[g] = kept("first_m%d" % g, [P, 2, PASS], BF16)
+            sync.dma_start(out=first_m[g][:], in_=m_rows[0][:, 0:2, PASS * g : PASS * (g + 1)])
+
+        def load_m(k):
+            m_sb[k] = streamed("m", [P, 2, NODES], BF16, 4)
+            t = 2 * (k % 2)
+            sync.dma_start(out=m_sb[k][:], in_=m_rows[k // 2][:, t : t + 2, :])
 
         def load_g(q):
-            gsb[q] = kt("g_%d" % q, [P, PACK, D], BF16)
-            sync.dma_start(out=gsb[q][:], in_=g_v[q])
-
-        def load_M(k):
-            Mk[k] = wt("M", [P, 2, NODES], BF16, 4)
-            sync.dma_start(out=Mk[k][:], in_=M_v[k // 2][:, 2 * (k % 2) : 2 * (k % 2) + 2, :])
+            g_sb[q] = kept("g%d" % q, [P, PACK, D], BF16)
+            sync.dma_start(out=g_sb[q][:], in_=g_rows[q])
 
         def load_h(q):
-            hsb[q] = kt("h_%d" % q, [P, PACK, D], BF16)
-            sync.dma_start(out=hsb[q][:], in_=h_v[q])
+            h_sb[q] = kept("h%d" % q, [P, PACK, D], BF16)
+            sync.dma_start(out=h_sb[q][:], in_=h_rows[q])
 
-        M0 = {}
-
-        def load_M0(g):
-            M0[g] = kt("M0_%d" % g, [P, 2, 512], BF16)
-            sync.dma_start(out=M0[g][:], in_=M_v[0][:, 0:2, 512 * g : 512 * (g + 1)])
-
-        load_M0(0)
-        load_M0(1)
+        load_first_m(0)
+        load_first_m(1)
         load_g(0)
         load_g(1)
-        load_M0(2)
-        load_M0(3)
-        load_M(1)
+        load_first_m(2)
+        load_first_m(3)
+        load_m(1)
         load_g(2)
         load_g(3)
-        wsb = kt("wsb", [P, PACK, D], BF16)
-        sync.dma_start(out=wsb[:], in_=W_v)
-        load_M(2)
-        load_M(3)
-        load_M(4)
+        w_sb = kept("w", [P, PACK, D], BF16)
+        sync.dma_start(out=w_sb[:], in_=w_rows)
+        load_m(2)
+        load_m(3)
+        load_m(4)
         load_h(0)
         load_h(1)
 
-        thr = kt("thr", [P, Q, PACK], F32)
-        thr_i = kt("thr_i", [P, Q, PACK], I32)
-        thr_b = kt("thr_b", [P, Q, PACK], BF16)
-        wse = kt("wse", [P, Q, PACK], F32)
-        den = kt("den", [P, Q, PACK], F32)
-        rec = kt("rec", [P, Q, PACK], F32)
-        edge = kt("edge", [P, Q, PACK], F32)
-        fac = kt("fac", [P, Q, PACK], F32)
-        lone = kt("lone", [P, Q, PACK], F32)
-        nb = kt("nb", [P, Q, PACK], F32)
-        vec.tensor_scalar(out=thr[:], in0=cs[:], scalar1=1e-8, scalar2=1e-6, op0=ALU.add, op1=ALU.mult)
-        vec.tensor_scalar(out=wse[:], in0=ws[:], scalar1=1e-8, scalar2=None, op0=ALU.add)
-        vec.tensor_scalar(out=thr_i[:], in0=thr[:].bitcast(I32), scalar1=-65536, scalar2=None, op0=ALU.bitwise_and)
-        vec.scalar_tensor_tensor(out=den[:], in0=cs[:], scalar=1e-8, in1=wse[:], op0=ALU.add, op1=ALU.mult)
-        vec.tensor_copy(out=thr_b[:], in_=thr_i[:].bitcast(F32))
-        vec.reciprocal(out=rec[:], in_=den[:])
-        vec.tensor_scalar(out=edge[:], in0=ws[:], scalar1=0.0, scalar2=None, op0=ALU.is_gt)
-        vec.tensor_scalar(out=lone[:], in0=ws[:], scalar1=0.0, scalar2=None, op0=ALU.is_le)
-        vec.tensor_tensor(out=fac[:], in0=rec[:], in1=edge[:], op=ALU.mult)
-        vec.tensor_scalar(out=nb[:], in0=thr_i[:].bitcast(F32), scalar1=-BIG, scalar2=None, op0=ALU.mult)
+        limit = kept("limit", [P, PASSES, PACK], F32)
+        limit_bits = kept("limit_bits", [P, PASSES, PACK], I32)
+        limit_bf = kept("limit_bf", [P, PASSES, PACK], BF16)
+        ws_eps = kept("ws_eps", [P, PASSES, PACK], F32)
+        product = kept("product", [P, PASSES, PACK], F32)
+        inverse = kept("inverse", [P, PASSES, PACK], F32)
+        has_edge = kept("has_edge", [P, PASSES, PACK], F32)
+        factor = kept("factor", [P, PASSES, PACK], F32)
+        no_edge = kept("no_edge", [P, PASSES, PACK], F32)
+        cut_bias = kept("cut_bias", [P, PASSES, PACK], F32)
+        vec.tensor_scalar(out=limit[:], in0=cs[:], scalar1=EPS, scalar2=THRESHOLD, op0=ALU.add, op1=ALU.mult)
+        vec.tensor_scalar(out=ws_eps[:], in0=ws[:], scalar1=EPS, scalar2=None, op0=ALU.add)
+        vec.tensor_scalar(out=limit_bits[:], in0=limit[:].bitcast(I32), scalar1=-65536, scalar2=None, op0=ALU.bitwise_and)
+        vec.scalar_tensor_tensor(out=product[:], in0=cs[:], scalar=EPS, in1=ws_eps[:], op0=ALU.add, op1=ALU.mult)
+        vec.tensor_copy(out=limit_bf[:], in_=limit_bits[:].bitcast(F32))
+        vec.reciprocal(out=inverse[:], in_=product[:])
+        vec.tensor_scalar(out=has_edge[:], in0=ws[:], scalar1=0.0, scalar2=None, op0=ALU.is_gt)
+        vec.tensor_scalar(out=no_edge[:], in0=ws[:], scalar1=0.0, scalar2=None, op0=ALU.is_le)
+        vec.tensor_tensor(out=factor[:], in0=inverse[:], in1=has_edge[:], op=ALU.mult)
+        vec.tensor_scalar(out=cut_bias[:], in0=limit_bits[:].bitcast(F32), scalar1=-STEEP, scalar2=None, op0=ALU.mult)
 
-        tr = {}
-        mask = {}
-        xm = {}
-        mcode, mscale = {}, {}
-
-        def T(k, g):
-            b = bank("tr%d" % g, [P, 2, R])
-            for tl in range(2):
-                if k == 0:
-                    words = M0[g][:, tl, :].bitcast(F32)
-                    off = 0
-                else:
-                    words = Mk[k][:, tl, :].bitcast(F32)
-                    off = 256 * g
-                for u in range(2):
-                    pe.transpose(b[:, u, P * tl : P * (tl + 1)], words[:, off + u : off + 256 : 2], ident[:])
-            tr[k, g] = b
-
-        def halves(k, g, a, b):
-            words = tr[k, g][:].rearrange("p u r -> p (u r)").bitcast(BF16)
-            return words.rearrange("p (u r e) -> p u r e", u=2, e=2)[:, :, a:b, :].rearrange("p u r e -> p r u e")
-
-        def GT(k, g, a=0, b=R):
-            if (k, g) in S_BANKS:
-                return
-            if a == 0:
-                mask[k, g] = wt("mask", [P, R, PACK], BF16, 4)
-            lim = thr_b[:, g, :].rearrange("p (u e) -> p u e", u=2).unsqueeze(1).to_broadcast([P, b - a, 2, 2])
-            vec.tensor_tensor(
-                out=mask[k, g][:, a:b, :].rearrange("p r (u e) -> p r u e", u=2), in0=halves(k, g, a, b), in1=lim, op=ALU.is_gt,
-            )
-
-        def LIM(k, g):
-            s = wt("slim", [P, 2, R, 2], BF16, 4)
-            src = tr[k, g][:].rearrange("p u r -> p (u r)").bitcast(BF16).rearrange("p (u r e) -> p u r e", u=2, e=2)
+        def turn(out, words):
             for u in range(2):
-                for e in range(2):
-                    j = 2 * u + e
-                    act.activation(out=s[:, u, :, e], in_=src[:, u, :, e], func=ACTF.Relu, scale=BIG, bias=nb[:, g, j : j + 1])
-            mask[k, g] = s
+                pe.transpose(out[:, u, :], words[:, u:256:2], identity[:])
 
-        def MUL(k, g, a=0, b=R):
-            if a == 0:
-                xm[k, g] = wt("xm", [P, R, PACK], BF16, 4)
-            if (k, g) in S_BANKS:
-                m, op = mask[k, g][:, :, a:b, :].rearrange("p u r e -> p r u e"), ALU.min
-            else:
-                m, op = mask[k, g][:, a:b, :].rearrange("p r (u e) -> p r u e", u=2), ALU.mult
-            vec.tensor_tensor(
-                out=xm[k, g][:, a:b, :].rearrange("p r (u e) -> p r u e", u=2), in0=halves(k, g, a, b), in1=m, op=op,
-            )
-
-        def MQ(k, g, a=0, b=R):
-            if k not in mcode:
-                mcode[k] = wt("mcode", [P, Q, R], U32, 3)
-                mscale[k] = wt("mscale", [P, Q, R], U8, 3)
-            vec.quantize_mx(
-                out=mcode[k][:, g, a:b].bitcast(E4M3),
-                scales=mscale[k][:, g, a:b],
-                in_=xm[k, g][:, a:b, :].rearrange("p r j -> p (r j)"),
-            )
-
-        def quant(name, src, width, fmt):
-            code = kt(name + "_c", [P, width], U32)
-            scale = kt(name + "_s", [P, width], U8)
-            vec.quantize_mx(out=code[:].bitcast(fmt), scales=scale[:], in_=src[:].rearrange("p c j -> p (c j)"))
-            return code, scale
-
-        def interleave_act(dst, src, a, b):
+        def straighten(out, turned):
             act.copy(
+                out=out.rearrange("p r t -> p (r t)").bitcast(F32).rearrange("p (r u) -> p r u", u=2),
+                in_=turned.rearrange("p u r -> p r u"),
+            )
+
+        def interleave(engine_copy, dst, src, a, b):
+            engine_copy(
                 out=dst[:, a:b, :].rearrange("p (c i) t -> p c t i", i=4),
                 in_=src[:, :, a:b].rearrange("p t (c i) -> p c t i", i=4),
             )
 
-        def interleave_gps(dst, src, a, b):
-            gps.tensor_scalar(
-                out=dst[:, a:b, :], in0=src[:, :, a:b].rearrange("p t d -> p d t"),
-                scalar1=1.0, scalar2=0.0, op0=ALU.mult, op1=ALU.add,
-            )
-
-        def interleave_vec(dst, src, a, b):
-            vec.tensor_copy(
-                out=dst[:, a:b, :].rearrange("p (c i) t -> p c t i", i=4),
-                in_=src[:, :, a:b].rearrange("p t (c i) -> p c t i", i=4),
-            )
-
-        zs, zi, z = {}, {}, {}
-
-        def DS(q):
-            t = wt("zs", [P, PACK, D], BF16, 2)
-            for j in range(PACK):
-                vec.tensor_scalar(out=t[:, j, :], in0=gsb[q][:, j, :], scalar1=fac[:, q, j : j + 1], scalar2=None, op0=ALU.mult)
-            zs[q] = t
-
-        def DI(q):
-            t = wt("zi", [P, D, PACK], BF16, 3)
-            zi[q] = t
-            if q % 2 == 0:
-                interleave_act(t, zs[q], 0, D)
-            else:
-                for a in range(0, D, 128):
-                    interleave_gps(t, zs[q], a, a + 128)
-
-        def DQ(q):
-            z[q] = quant("z%d" % q, zi[q], D, E5M2)
-
-        dh = {}
-
-        def MM(k, tl, gs):
-            if gs[0] == 0:
-                dh[k, tl] = bank("dh%d" % tl, [P, D])
-            cols = slice(P * tl, P * (tl + 1))
-            for g in gs:
-                pe.matmul_mx(
-                    out=dh[k, tl][:],
-                    lhsT=mcode[k][:, g, cols].bitcast(E4M3),
-                    lhsT_scale=mscale[k][:, g, cols],
-                    rhs=z[g][0][:].bitcast(E5M2),
-                    rhs_scale=z[g][1][:],
-                    start=(g == 0),
-                    stop=(g == Q - 1),
+        def interleave_on_gpsimd(dst, src):
+            for a in range(0, D, P):
+                gps.tensor_scalar(
+                    out=dst[:, a : a + P, :], in0=src[:, :, a : a + P].rearrange("p t d -> p d t"),
+                    scalar1=1.0, scalar2=0.0, op0=ALU.mult, op1=ALU.add,
                 )
 
-        dz1 = {}
+        def quantise(name, src, fmt):
+            codes = kept(name + "_codes", [P, D], U32)
+            scales = kept(name + "_scales", [P, D], U8)
+            vec.quantize_mx(out=codes[:].bitcast(fmt), scales=scales[:], in_=src[:].rearrange("p c t -> p (c t)"))
+            return codes, scales
 
-        def STT(k, tl):
-            q, t = k // 2, 2 * (k % 2) + tl
+        def multiply(out, left, left_fmt, cols, right, right_fmt, start, stop):
+            pe.matmul_mx(
+                out=out, lhsT=left[0][:, cols].bitcast(left_fmt), lhsT_scale=left[1][:, cols],
+                rhs=right[0][:].bitcast(right_fmt), rhs_scale=right[1][:], start=start, stop=stop,
+            )
+
+        turned, mask, masked, mm = {}, {}, {}, {}
+
+        def turn_m(k, g):
+            turned[k, g] = bank("turn%d" % g, [P, 2, ROWS])
+            for i in range(2):
+                if k == 0:
+                    words = first_m[g][:, i, :].bitcast(F32)
+                else:
+                    words = m_sb[k][:, i, PASS * g : PASS * (g + 1)].bitcast(F32)
+                turn(turned[k, g][:, :, P * i : P * (i + 1)], words)
+            if g in CUT_ON_SCALAR[k]:
+                cut_on_scalar(k, g)
+
+        def values(k, g):
+            return turned[k, g][:].rearrange("p u r -> p (u r)").bitcast(BF16).rearrange("p (u r e) -> p u r e", u=2, e=2)
+
+        def cut_on_scalar(k, g):
+            cut = streamed("cut", [P, 2, ROWS, 2], BF16, 4)
+            x = values(k, g)
+            for u in range(2):
+                for e in range(2):
+                    t = 2 * u + e
+                    act.activation(out=cut[:, u, :, e], in_=x[:, u, :, e], func=ACT.Relu, scale=STEEP, bias=cut_bias[:, g, t : t + 1])
+            mask[k, g] = cut
+
+        def compare(k, g, a=0, b=ROWS):
+            if g in CUT_ON_SCALAR[k]:
+                return
+            if a == 0:
+                mask[k, g] = streamed("mask", [P, ROWS, PACK], BF16, 4)
+            limits = limit_bf[:, g, :].rearrange("p (u e) -> p u e", u=2).unsqueeze(1).to_broadcast([P, b - a, 2, 2])
+            vec.tensor_tensor(
+                out=mask[k, g][:, a:b, :].rearrange("p r (u e) -> p r u e", u=2),
+                in0=values(k, g)[:, :, a:b, :].rearrange("p u r e -> p r u e"), in1=limits, op=ALU.is_gt,
+            )
+
+        def apply_mask(k, g, a=0, b=ROWS):
+            if a == 0:
+                masked[k, g] = streamed("masked", [P, ROWS, PACK], BF16, 4)
+            if g in CUT_ON_SCALAR[k]:
+                other, op = mask[k, g][:, :, a:b, :].rearrange("p u r e -> p r u e"), ALU.min
+            else:
+                other, op = mask[k, g][:, a:b, :].rearrange("p r (u e) -> p r u e", u=2), ALU.mult
+            vec.tensor_tensor(
+                out=masked[k, g][:, a:b, :].rearrange("p r (u e) -> p r u e", u=2),
+                in0=values(k, g)[:, :, a:b, :].rearrange("p u r e -> p r u e"), in1=other, op=op,
+            )
+
+        def mask_two(k, g):
+            compare(k, g)
+            compare(k, g + 1)
+            apply_mask(k, g)
+            apply_mask(k, g + 1)
+
+        def quantise_mm(k, g, a=0, b=ROWS):
+            if k not in mm:
+                mm[k] = (streamed("mm_codes", [P, PASSES, ROWS], U32, 3), streamed("mm_scales", [P, PASSES, ROWS], U8, 3))
+            codes, scales = mm[k]
+            vec.quantize_mx(
+                out=codes[:, g, a:b].bitcast(E4M3), scales=scales[:, g, a:b],
+                in_=masked[k, g][:, a:b, :].rearrange("p r t -> p (r t)"),
+            )
+
+        dz2_rows, dz2_sorted, dz2 = {}, {}, {}
+
+        def scale_dz2(q):
+            dz2_rows[q] = streamed("dz2_rows", [P, PACK, D], BF16, 2)
+            for t in range(PACK):
+                vec.tensor_scalar(
+                    out=dz2_rows[q][:, t, :], in0=g_sb[q][:, t, :], scalar1=factor[:, q, t : t + 1], scalar2=None, op0=ALU.mult,
+                )
+            dz2_sorted[q] = streamed("dz2_sorted", [P, D, PACK], BF16, 3)
+            if q % 2 == 0:
+                interleave(act.copy, dz2_sorted[q], dz2_rows[q], 0, D)
+            else:
+                interleave_on_gpsimd(dz2_sorted[q], dz2_rows[q])
+
+        def quantise_dz2(q):
+            dz2[q] = quantise("dz2_%d" % q, dz2_sorted[q], E5M2)
+
+        dh, dz1 = {}, {}
+
+        def place(k, i):
+            return k // 2, 2 * (k % 2) + i
+
+        def multiply_dh(k, i, passes=range(PASSES)):
+            if passes[0] == 0:
+                dh[k, i] = bank("dh%d" % i, [P, D])
+            for g in passes:
+                left = (mm[k][0][:, g, :], mm[k][1][:, g, :])
+                multiply(dh[k, i][:], left, E4M3, slice(P * i, P * (i + 1)), dz2[g], E5M2, g == 0, g == PASSES - 1)
+
+        def add_g(k, i):
+            q, t = place(k, i)
             if t == 0:
-                dz1[q] = wt("dz1", [P, PACK, D], BF16, 2)
+                dz1[q] = streamed("dz1", [P, PACK, D], BF16, 2)
             vec.scalar_tensor_tensor(
-                out=dz1[q][:, t, :], in0=gsb[q][:, t, :], scalar=lone[:, q, t : t + 1], in1=dh[k, tl][:],
+                out=dz1[q][:, t, :], in0=g_sb[q][:, t, :], scalar=no_edge[:, q, t : t + 1], in1=dh[k, i][:],
                 op0=ALU.mult, op1=ALU.add,
             )
 
-        dhs = {}
+        dz1_turned, dz1_f, dz1_fq, out_bank, out_sb = {}, {}, {}, {}, {}
 
-        def on_gps(k, tl):
-            return GADD(k, tl)
+        def turn_dz1(k, i):
+            q, t = place(k, i)
+            if i == 0:
+                dz1_turned[k] = bank("xt", [P, 2, ROWS])
+            turn(dz1_turned[k][:, :, P * i : P * (i + 1)], dz1[q][:, t, :].bitcast(F32))
 
-        def MG(q, n):
-            for t in range(PACK):
-                if not on_gps(2 * q + t // 2, t % 2):
-                    continue
-                if n == 1:
-                    vec.tensor_scalar(out=gsb[q][:, t, :], in0=gsb[q][:, t, :], scalar1=lone[:, q, t : t + 1], scalar2=None, op0=ALU.mult)
-                    continue
-                act.activation(out=gsb[q][:, t, :], in_=gsb[q][:, t, :], func=ACTF.Copy, scale=lone[:, q, t : t + 1])
-
-        def EV(k, tl):
-            dhs[k, tl] = wt("dhs", [P, D], F32, 3)
-            act.copy(out=dhs[k, tl][:], in_=dh[k, tl][:])
-
-        def EVX(k, tl):
-            if on_gps(k, tl):
-                EV(k, tl)
-
-        def ADD(k, tl):
-            q, t = k // 2, 2 * (k % 2) + tl
-            if not on_gps(k, tl):
-                STT(k, tl)
-                return
-            if t == 0:
-                dz1[q] = wt("dz1", [P, PACK, D], BF16, 2)
-            gps.tensor_tensor(out=dz1[q][:, t, :], in0=dhs[k, tl][:], in1=gsb[q][:, t, :], op=ALU.add)
-
-        xt, xg, dxc = {}, {}, {}
-
-        def X(k, tl):
-            q, t = k // 2, 2 * (k % 2) + tl
-            if tl == 0:
-                xt[k] = bank("xt", [P, 2, R])
-            words = dz1[q][:, t, :].bitcast(F32)
-            for u in range(2):
-                pe.transpose(xt[k][:, u, P * tl : P * (tl + 1)], words[:, u:256:2], ident[:])
-
-        def XC(k, a=0, b=R):
+        def straighten_dz1(k, a=0, b=ROWS):
             if a == 0:
-                xg[k] = wt("xg", [P, R, PACK], BF16, 2)
-            act.copy(
-                out=xg[k][:, a:b, :].rearrange("p r j -> p (r j)").bitcast(F32).rearrange("p (r u) -> p r u", u=2),
-                in_=xt[k][:, :, a:b].rearrange("p u r -> p r u"),
+                dz1_f[k] = streamed("dz1_f", [P, ROWS, PACK], BF16, 2)
+            straighten(dz1_f[k][:, a:b, :], dz1_turned[k][:, :, a:b])
+
+        def quantise_dz1_f(k, a=0, b=ROWS):
+            if a == 0:
+                dz1_fq[k] = (streamed("dz1_f_codes", [P, ROWS], U32, 4), streamed("dz1_f_scales", [P, ROWS], U8, 4))
+            codes, scales = dz1_fq[k]
+            vec.quantize_mx(
+                out=codes[:, a:b].bitcast(E5M2), scales=scales[:, a:b], in_=dz1_f[k][:, a:b, :].rearrange("p r t -> p (r t)"),
             )
 
-        def XQ(k, a=0, b=R):
-            if a == 0:
-                dxc[k] = (wt("dx_c", [P, R], U32, 4), wt("dx_s", [P, R], U8, 4))
-            code, scale = dxc[k]
-            vec.quantize_mx(out=code[:, a:b].bitcast(E5M2), scales=scale[:, a:b], in_=xg[k][:, a:b, :].rearrange("p r j -> p (r j)"))
+        def multiply_out0(k, i, where):
+            out_bank[k, i] = bank(where, [P, D])
+            multiply(out_bank[k, i][:], dz1_fq[k], E5M2, slice(P * i, P * (i + 1)), wq, E4M3, True, True)
 
-        ob, ops = {}, {}
+        def empty_out0(k, i):
+            if i == 0:
+                out_sb[k] = streamed("out_sb", [P, 2, D], F32, 3)
+            act.copy(out=out_sb[k][:, i, :], in_=out_bank[k, i][:])
 
-        def O(k, tl, tag):
-            b = bank(tag, [P, D])
-            cols = slice(P * tl, P * (tl + 1))
-            pe.matmul_mx(
-                out=b[:], lhsT=dxc[k][0][:, cols].bitcast(E5M2), lhsT_scale=dxc[k][1][:, cols],
-                rhs=wq[0][:].bitcast(E4M3), rhs_scale=wq[1][:], start=True, stop=True,
-            )
-            ops[k, tl] = b
+        def store_out0(k):
+            q, t = place(k, 0)
+            sync.dma_start(out=o_rows[q][:, t : t + 2, :], in_=out_sb[k][:])
 
-        def OE(k, tl, eng):
-            if tl == 0:
-                ob[k] = wt("ob", [P, 2, D], F32, 3)
-            if eng == "act":
-                act.copy(out=ob[k][:, tl, :], in_=ops[k, tl][:])
-            else:
-                vec.tensor_copy(out=ob[k][:, tl, :], in_=ops[k, tl][:])
+        def finish_out0(k):
+            empty_out0(k, 0)
+            empty_out0(k, 1)
+            store_out0(k)
 
-        def OS(k):
-            h = 2 * (k % 2)
-            sync.dma_start(out=o_v[k // 2][:, h : h + 2, :], in_=ob[k][:])
+        dz1_n, dz1_nq, h_n, hq, sums = {}, {}, {}, {}, {}
 
-        di, dq, hq, hi = {}, {}, {}, {}
+        def interleave_dz1(q):
+            dz1_n[q] = streamed("dz1_n", [P, D, PACK], BF16, 2)
+            interleave_on_gpsimd(dz1_n[q], dz1[q])
 
-        def IQ(q):
-            dq[q] = quant("d%d" % q, di[q], D, E5M2)
+        def quantise_dz1_n(q):
+            dz1_nq[q] = quantise("dz1_n%d" % q, dz1_n[q], E5M2)
 
-        def HI(q, half_no):
-            if half_no == 0:
-                hi[q] = wt("hi", [P, D, PACK], BF16, 1)
-            for a in (256 * half_no, 256 * half_no + 128):
-                interleave_gps(hi[q], hsb[q], a, a + 128)
+        def interleave_h(q):
+            h_n[q] = streamed("h_n", [P, D, PACK], BF16, 1)
+            interleave_on_gpsimd(h_n[q], h_sb[q])
 
-        def DZI(q, half_no):
-            if half_no == 0:
-                di[q] = wt("di", [P, D, PACK], BF16, 2)
-            interleave_act(di[q], dz1[q], 256 * half_no, 256 * half_no + 256)
+        def interleave_last_h(half):
+            q = PASSES - 1
+            if half == 0:
+                h_n[q] = kept("h_n_last", [P, D, PACK], BF16)
+            interleave(act.copy, h_n[q], h_sb[q], ROWS * half, ROWS * (half + 1))
 
-        def HQ(q):
-            hq[q] = quant("h%dq" % q, hi[q], D, E4M3)
+        def quantise_h(q):
+            hq[q] = quantise("h%dq" % q, h_n[q], E4M3)
 
-        oc = {}
-
-        def OUT1(c, q):
+        def multiply_out1(c, q):
             if q == 0:
-                oc[c] = bank("tr%d" % c, [P, D])
-            cols = slice(P * c, P * (c + 1))
-            pe.matmul_mx(
-                out=oc[c][:], lhsT=hq[q][0][:, cols].bitcast(E4M3), lhsT_scale=hq[q][1][:, cols],
-                rhs=dq[q][0][:].bitcast(E5M2), rhs_scale=dq[q][1][:], start=(q == 0), stop=(q == Q - 1),
-            )
+                sums[c] = bank("turn%d" % c, [P, D])
+            multiply(sums[c][:], hq[q], E4M3, slice(P * c, P * (c + 1)), dz1_nq[q], E5M2, q == 0, q == PASSES - 1)
 
-        wg = kt("wg", [P, D, PACK], BF16)
-        wb = []
+        w_f = kept("w_f", [P, D, PACK], BF16)
 
-        def WT(b):
-            t = bank("xt" if b == 0 else "o", [P, 2, R])
-            for m in range(2):
-                words = wsb[:, 2 * b + m, :].bitcast(F32)
-                for u in range(2):
-                    pe.transpose(t[:, u, P * m : P * (m + 1)], words[:, u:256:2], ident[:])
-            wb.append(t)
+        def turn_w():
+            halves = []
+            for n, where in enumerate(("xt", "o")):
+                b = bank(where, [P, 2, ROWS])
+                for i in range(2):
+                    turn(b[:, :, P * i : P * (i + 1)], w_sb[:, 2 * n + i, :].bitcast(F32))
+                halves.append(b)
+            for n in range(2):
+                straighten(w_f[:, ROWS * n : ROWS * (n + 1), :], halves[n][:])
 
-        def WC(b):
-            act.copy(
-                out=wg[:, R * b : R * (b + 1), :].rearrange("p r j -> p (r j)").bitcast(F32).rearrange("p (r u) -> p r u", u=2),
-                in_=wb[b][:].rearrange("p u r -> p r u"),
-            )
-
-        S_BANKS = set([(k, 0) for k in range(NS0, NS1)] + [(1,1),(2,0),(2,1),(2,2),(3,2),(4,2),(5,2),(6,2),(7,0)])
-
-        def half(k, g0):
-            for g in (g0, g0 + 1):
-                if (k, g) not in S_BANKS:
-                    GT(k, g)
-            MUL(k, g0)
-            MUL(k, g0 + 1)
-
-        pieces = {
-            2: [(HI, 0, 0), (HI, 0, 1)],
-            3: [(HI, 1, 0), (HI, 1, 1), (DZI, 0, 0), (DZI, 0, 1)],
-            4: [(HI, 2, 0), (HI, 2, 1)],
-            5: [(HI, 3, 0), (HI, 3, 1), (DZI, 1, 0)],
-            6: [(DZI, 1, 1)],
-        }
-        quants = {2: [(HQ, 0)], 3: [(HQ, 1)], 4: [(IQ, 0), (HQ, 2)], 5: [(HQ, 3)], 6: []}
-
-        def run_pieces(k):
-            for f, q, n in pieces[k]:
-                if n is None:
-                    f(q)
-                else:
-                    f(q, n)
-
-        def TL(k, g):
-            T(k, g)
-            if (k, g) in S_BANKS:
-                LIM(k, g)
-
-        for g in range(Q):
-            T(0, g)
-        GT(0, 0)
-        GT(0, 1)
-        DS(0)
-        DI(0)
-        MUL(0, 0)
-        MUL(0, 1)
-        TL(1, 0)
-        TL(1, 1)
-        DS(1)
-        DI(1)
-        half(0, 2)
-        TL(1, 2)
-        TL(1, 3)
-        for g in range(Q):
-            MQ(0, g)
-        load_M(5)
+        for g in range(PASSES):
+            turn_m(0, g)
+        compare(0, 0)
+        compare(0, 1)
+        scale_dz2(0)
+        apply_mask(0, 0)
+        apply_mask(0, 1)
+        turn_m(1, 0)
+        turn_m(1, 1)
+        scale_dz2(1)
+        mask_two(0, 2)
+        turn_m(1, 2)
+        turn_m(1, 3)
+        for g in range(PASSES):
+            quantise_mm(0, g)
+        load_m(5)
         load_h(2)
         load_h(3)
-        DS(2)
-        DI(2)
-        half(1, 0)
-        DS(3)
-        DI(3)
-        WT(0)
-        WT(1)
-        WC(0)
-        WC(1)
-        TL(2, 0)
-        TL(2, 1)
-        DQ(0)
-        DQ(1)
-        half(1, 2)
-        DQ(2)
-        DQ(3)
-        TL(2, 2)
-        TL(2, 3)
-        MM(0, 0, range(Q))
-        MM(0, 1, range(Q))
-        for g in range(Q):
-            MQ(1, g)
-        load_M(6)
-        for k in range(2, STEPS - 1):
+
+        scale_dz2(2)
+        mask_two(1, 0)
+        scale_dz2(3)
+        turn_w()
+        turn_m(2, 0)
+        turn_m(2, 1)
+        quantise_dz2(0)
+        quantise_dz2(1)
+        multiply_dh(0, 0, (0, 1))
+        multiply_dh(0, 1, (0, 1))
+        mask_two(1, 2)
+        quantise_dz2(2)
+        quantise_dz2(3)
+        turn_m(2, 2)
+        turn_m(2, 3)
+        multiply_dh(0, 0, (2, 3))
+        multiply_dh(0, 1, (2, 3))
+        for g in range(PASSES):
+            quantise_mm(1, g)
+        load_m(6)
+
+        mask_two(2, 0)
+        turn_m(3, 0)
+        turn_m(3, 1)
+        compare(2, 2)
+        compare(2, 3)
+        add_g(0, 0)
+        multiply_dh(1, 0)
+        interleave_h(0)
+        apply_mask(2, 2)
+        apply_mask(2, 3)
+        add_g(0, 1)
+        multiply_dh(1, 1)
+        turn_dz1(0, 0)
+        turn_dz1(0, 1)
+        straighten_dz1(0)
+        turn_m(3, 2)
+        turn_m(3, 3)
+        quantise_mm(2, 0)
+        quantise_mm(2, 1)
+        add_g(1, 0)
+        quantise_mm(2, 2)
+        quantise_mm(2, 3)
+        add_g(1, 1)
+        load_m(7)
+
+        for k in range(3, LAST):
             if k > 3:
-                OE(k - 4, 0, "act")
-                OE(k - 4, 1, "act")
-                OS(k - 4)
-            MM(k - 1, 0, range(Q))
+                finish_out0(k - 4)
+            multiply_dh(k - 1, 0)
+            turn_dz1(k - 2, 0)
+            turn_dz1(k - 2, 1)
+            straighten_dz1(k - 2)
+            mask_two(k, 0)
+            if k > 3:
+                add_g(k - 1, 0)
+            turn_m(k + 1, 0)
+            turn_m(k + 1, 1)
             if k == 3:
-                XQ(0)
-                wq = quant("w", wg, D, E4M3)
-            if k > 2:
-                X(k - 2, 0)
-                X(k - 2, 1)
-                XC(k - 2)
-            half(k, 0)
-            if k == 2:
-                STT(0, 0)
-                STT(0, 1)
-            STT(k - 1, 0)
-            TL(k + 1, 0)
-            TL(k + 1, 1)
-            if k == 2:
-                X(0, 0)
-                X(0, 1)
-                XC(0)
-            run_pieces(k)
-            MM(k - 1, 1, range(Q))
-            half(k, 2)
-            TL(k + 1, 2)
-            TL(k + 1, 3)
-            if k > 2:
-                O(k - 3, 0, "o")
-                O(k - 3, 1, "dh1")
-            if k > 2:
-                XQ(k - 2)
-            MQ(k, 0)
-            MQ(k, 1)
-            STT(k - 1, 1)
-            MQ(k, 2)
-            MQ(k, 3)
-            for f, q in quants[k]:
-                f(q)
-            if k == 2:
-                load_M(7)
-        OE(3, 0, "act")
-        OE(3, 1, "act")
-        OS(3)
-        MM(6, 0, range(Q))
-        EVX(6, 0)
-        X(5, 0)
-        X(5, 1)
-        XC(5)
-        MM(6, 1, range(Q))
-        EVX(6, 1)
-        for g in range(Q):
-            GT(7, g, 0, P)
-        DZI(2, 0)
-        ADD(6, 0)
-        for g in range(Q):
-            MUL(7, g, 0, P)
-        DZI(2, 1)
-        O(4, 0, "o")
-        OE(4, 0, "act")
-        O(4, 1, "dh1")
-        OE(4, 1, "act")
-        OS(4)
-        for g in range(Q):
-            MQ(7, g, 0, P)
-        ADD(6, 1)
-        MM(7, 0, range(Q))
-        X(6, 0)
-        X(6, 1)
-        XC(6)
-        XQ(5)
-        IQ(1)
-        O(5, 0, "o")
-        O(5, 1, "dh1")
-        OE(5, 0, "act")
-        OE(5, 1, "act")
-        OS(5)
-        for g in range(Q):
-            GT(7, g, P, R)
-        STT(7, 0)
-        X(7, 0)
-        XC(7, 0, P)
-        for g in range(Q):
-            MUL(7, g, P, R)
-        XQ(6)
-        for c in range(2):
-            OUT1(c, 0)
-            OUT1(c, 1)
-        for g in range(Q):
-            MQ(7, g, P, R)
-            MM(7, 1, [g])
-        IQ(2)
-        XQ(7, 0, P)
-        OUT1(2, 0)
-        OUT1(2, 1)
-        STT(7, 1)
-        X(7, 1)
-        XC(7, P, R)
-        di[3] = wt("di", [P, D, PACK], BF16, 2)
-        interleave_vec(di[3], dz1[3], 0, VSHARE)
-        interleave_act(di[3], dz1[3], VSHARE, D)
-        O(6, 0, "o")
-        O(6, 1, "dh0")
-        OE(6, 0, "act")
-        OE(6, 1, "act")
-        OS(6)
-        OUT1(3, 0)
-        OUT1(3, 1)
-        O(7, 0, "dh1")
-        OUT1(0, 2)
-        OUT1(1, 2)
-        XQ(7, P, R)
-        OUT1(2, 2)
-        O(7, 1, "xt")
-        OUT1(3, 2)
-        IQ(3)
-        OE(7, 0, "act")
-        OE(7, 1, "vec")
-        OS(7)
-        for c in range(4):
-            OUT1(c, 3)
-            t = kt("oc%d" % c, [P, D], F32)
-            if c % 2 == 0:
-                act.copy(out=t[:], in_=oc[c][:])
+                interleave_dz1(0)
+            elif k == 4:
+                interleave_h(1)
+                interleave_last_h(0)
+            elif k == 5:
+                interleave_dz1(1)
+                interleave_last_h(1)
             else:
-                vec.tensor_copy(out=t[:], in_=oc[c][:])
-            sync.dma_start(out=out_1[P * c : P * (c + 1), :], in_=t[:])
+                interleave_h(2)
+            multiply_dh(k - 1, 1)
+            mask_two(k, 2)
+            turn_m(k + 1, 2)
+            turn_m(k + 1, 3)
+            if k == 3:
+                add_g(2, 0)
+                quantise_dz1_f(0)
+                wq = quantise("w_f", w_f, E4M3)
+            multiply_out0(k - 3, 0, "o")
+            multiply_out0(k - 3, 1, "dh1")
+            quantise_dz1_f(k - 2)
+            quantise_mm(k, 0)
+            quantise_mm(k, 1)
+            if k % 2 == 1:
+                add_g(k - 1, 1)
+            quantise_mm(k, 2)
+            quantise_mm(k, 3)
+            if k % 2 == 1:
+                quantise_h((k - 3) // 2)
+            else:
+                quantise_dz1_n((k - 4) // 2)
+                add_g(k - 1, 1)
+
+        interleave_dz1(2)
+        finish_out0(3)
+        multiply_dh(6, 0)
+        turn_dz1(5, 0)
+        turn_dz1(5, 1)
+        straighten_dz1(5)
+        multiply_dh(6, 1)
+        for g in range(PASSES):
+            compare(LAST, g, 0, P)
+        add_g(6, 0)
+        for g in range(PASSES):
+            apply_mask(LAST, g, 0, P)
+        multiply_out0(4, 0, "o")
+        empty_out0(4, 0)
+        multiply_out0(4, 1, "dh1")
+        empty_out0(4, 1)
+        store_out0(4)
+        for g in range(PASSES):
+            quantise_mm(LAST, g, 0, P)
+        add_g(6, 1)
+        multiply_dh(LAST, 0)
+        turn_dz1(6, 0)
+        turn_dz1(6, 1)
+        straighten_dz1(6)
+        quantise_dz1_f(5)
+        quantise_h(2)
+        multiply_out0(5, 0, "o")
+        multiply_out0(5, 1, "dh1")
+        finish_out0(5)
+        for g in range(PASSES):
+            compare(LAST, g, P, ROWS)
+        add_g(LAST, 0)
+        quantise_dz1_f(6)
+        turn_dz1(LAST, 0)
+        straighten_dz1(LAST, 0, P)
+        multiply_out0(6, 0, "o")
+        multiply_out0(6, 1, "dh0")
+        finish_out0(6)
+        for g in range(PASSES):
+            apply_mask(LAST, g, P, ROWS)
+        multiply_out1(0, 0)
+        multiply_out1(0, 1)
+        for g in range(PASSES):
+            quantise_mm(LAST, g, P, ROWS)
+            multiply_dh(LAST, 1, (g,))
+        quantise_dz1_f(LAST, 0, P)
+        quantise_dz1_n(2)
+        multiply_out1(1, 0)
+        multiply_out1(1, 1)
+        multiply_out0(LAST, 0, "o")
+        empty_out0(LAST, 0)
+        sync.dma_start(out=o_rows[PASSES - 1][:, 2, :], in_=out_sb[LAST][:, 0, :])
+        add_g(LAST, 1)
+        turn_dz1(LAST, 1)
+        straighten_dz1(LAST, P, ROWS)
+        last_n = streamed("dz1_n", [P, D, PACK], BF16, 2)
+        dz1_n[PASSES - 1] = last_n
+        interleave(vec.tensor_copy, last_n, dz1[PASSES - 1], 0, VECTOR_COLUMNS)
+        interleave(act.copy, last_n, dz1[PASSES - 1], VECTOR_COLUMNS, D)
+        for c in (2, 3):
+            multiply_out1(c, 0)
+            multiply_out1(c, 1)
+        for c in range(3):
+            multiply_out1(c, 2)
+        quantise_dz1_f(LAST, P, ROWS)
+        quantise_h(PASSES - 1)
+        multiply_out0(LAST, 1, "dh1")
+        empty_out0(LAST, 1)
+        sync.dma_start(out=o_rows[PASSES - 1][:, 3, :], in_=out_sb[LAST][:, 1, :])
+        multiply_out1(3, 2)
+        quantise_dz1_n(PASSES - 1)
+        for c in range(D // P):
+            multiply_out1(c, PASSES - 1)
+            result = kept("out1_%d" % c, [P, D], F32)
+            if c % 2 == 0:
+                vec.tensor_copy(out=result[:], in_=sums[c][:])
+            else:
+                act.copy(out=result[:], in_=sums[c][:])
+            sync.dma_start(out=out_1[P * c : P * (c + 1), :], in_=result[:])

from contextlib import ExitStack

import concourse.mybir as mybir
from concourse.masks import make_identity

NODES, D = 2048, 512
FLOPS = 2 * NODES * NODES * D + 2 * (2 * NODES * D * D)
BYTES = 2 * (NODES * NODES + 2 * NODES * D + D * D) + 4 * 2 * NODES + 4 * (NODES * D + D * D)

F32 = mybir.dt.float32
BF16 = mybir.dt.bfloat16
I32 = mybir.dt.int32
U32 = mybir.dt.uint32
U8 = mybir.dt.uint8
E4M3 = mybir.dt.float8_e4m3fn_x4
E5M2 = mybir.dt.float8_e5m2_x4
ALU = mybir.AluOpType
ACT = mybir.ActivationFunctionType

P = 128
PACK = 4
PASS = P * PACK
PASSES = NODES // PASS
ROWS = 2 * P
STEPS = NODES // ROWS
LAST = STEPS - 1

THRESHOLD, EPS = 1e-6, 1e-8
STEEP = 1024.0

CUT_ON_SCALAR = {0: (), 1: (1,), 2: (0, 1, 2), 3: (0, 2), 4: (0, 2), 5: (0, 2), 6: (0, 2), 7: (0, 1)}
VECTOR_COLUMNS = 416


def tile_mobilitygnn_pb_v_kernel(tc, h1, mobility_matrix, W_in, b_in, col_sum, w_sum, grad_out, out_0, out_1):
    nc = tc.nc
    pe, vec, act, gps, sync = nc.tensor, nc.vector, nc.scalar, nc.gpsimd, nc.sync

    m_rows = mobility_matrix.rearrange("(g p t) i -> g p t i", g=PASSES, p=P)
    g_rows = grad_out.rearrange("(g p t) d -> g p t d", g=PASSES, p=P)
    h_rows = h1.rearrange("(g p t) h -> g p t h", g=PASSES, p=P)
    w_rows = W_in.rearrange("(m p) d -> p m d", p=P)
    o_rows = out_0.rearrange("(g p t) h -> g p t h", g=PASSES, p=P)
    col_sums = col_sum.rearrange("(g p t) -> p g t", g=PASSES, p=P)
    w_sums = w_sum.rearrange("(g p t) -> p g t", g=PASSES, p=P)

    with ExitStack() as ctx:
        keep = ctx.enter_context(tc.tile_pool(name="keep", bufs=1))
        stream = ctx.enter_context(tc.tile_pool(name="stream", bufs=2))
        psum = ctx.enter_context(tc.psum_pool(name="psum", bufs=1))
        ctx.enter_context(tc.manual_schedule())

        def kept(name, shape, dtype):
            return keep.tile(shape, dtype, name=name, tag=name, align_bytes=64)

        def streamed(name, shape, dtype, bufs):
            return stream.tile(shape, dtype, name=name, tag=name, bufs=bufs, align_bytes=64)

        def bank(name, shape):
            return psum.tile(shape, F32, name=name, tag=name)

        cs = kept("cs", [P, PASSES, PACK], F32)
        ws = kept("ws", [P, PASSES, PACK], F32)
        act.dma_start(out=cs[:], in_=col_sums)
        act.dma_start(out=ws[:], in_=w_sums)
        identity = kept("identity", [P, P], F32)
        make_identity(nc, identity[:])

        first_m, m_sb, g_sb, h_sb = {}, {}, {}, {}

        def load_first_m(g):
            first_m[g] = kept("first_m%d" % g, [P, 2, PASS], BF16)
            sync.dma_start(out=first_m[g][:], in_=m_rows[0][:, 0:2, PASS * g : PASS * (g + 1)])

        def load_m(k):
            m_sb[k] = streamed("m", [P, 2, NODES], BF16, 4)
            t = 2 * (k % 2)
            sync.dma_start(out=m_sb[k][:], in_=m_rows[k // 2][:, t : t + 2, :])

        def load_g(q):
            g_sb[q] = kept("g%d" % q, [P, PACK, D], BF16)
            sync.dma_start(out=g_sb[q][:], in_=g_rows[q])

        def load_h(q):
            h_sb[q] = kept("h%d" % q, [P, PACK, D], BF16)
            sync.dma_start(out=h_sb[q][:], in_=h_rows[q])

        load_first_m(0)
        load_first_m(1)
        load_g(0)
        load_g(1)
        load_first_m(2)
        load_first_m(3)
        load_m(1)
        load_g(2)
        load_g(3)
        w_sb = kept("w", [P, PACK, D], BF16)
        sync.dma_start(out=w_sb[:], in_=w_rows)
        load_m(2)
        load_m(3)
        load_m(4)
        load_h(0)
        load_h(1)

        limit = kept("limit", [P, PASSES, PACK], F32)
        limit_bits = kept("limit_bits", [P, PASSES, PACK], I32)
        limit_bf = kept("limit_bf", [P, PASSES, PACK], BF16)
        ws_eps = kept("ws_eps", [P, PASSES, PACK], F32)
        product = kept("product", [P, PASSES, PACK], F32)
        inverse = kept("inverse", [P, PASSES, PACK], F32)
        has_edge = kept("has_edge", [P, PASSES, PACK], F32)
        factor = kept("factor", [P, PASSES, PACK], F32)
        no_edge = kept("no_edge", [P, PASSES, PACK], F32)
        cut_bias = kept("cut_bias", [P, PASSES, PACK], F32)
        vec.tensor_scalar(out=limit[:], in0=cs[:], scalar1=EPS, scalar2=THRESHOLD, op0=ALU.add, op1=ALU.mult)
        vec.tensor_scalar(out=ws_eps[:], in0=ws[:], scalar1=EPS, scalar2=None, op0=ALU.add)
        vec.tensor_scalar(out=limit_bits[:], in0=limit[:].bitcast(I32), scalar1=-65536, scalar2=None, op0=ALU.bitwise_and)
        vec.scalar_tensor_tensor(out=product[:], in0=cs[:], scalar=EPS, in1=ws_eps[:], op0=ALU.add, op1=ALU.mult)
        vec.tensor_copy(out=limit_bf[:], in_=limit_bits[:].bitcast(F32))
        vec.reciprocal(out=inverse[:], in_=product[:])
        vec.tensor_scalar(out=has_edge[:], in0=ws[:], scalar1=0.0, scalar2=None, op0=ALU.is_gt)
        vec.tensor_scalar(out=no_edge[:], in0=ws[:], scalar1=0.0, scalar2=None, op0=ALU.is_le)
        vec.tensor_tensor(out=factor[:], in0=inverse[:], in1=has_edge[:], op=ALU.mult)
        vec.tensor_scalar(out=cut_bias[:], in0=limit_bits[:].bitcast(F32), scalar1=-STEEP, scalar2=None, op0=ALU.mult)

        def turn(out, words):
            for u in range(2):
                pe.transpose(out[:, u, :], words[:, u:256:2], identity[:])

        def straighten(out, turned):
            act.copy(
                out=out.rearrange("p r t -> p (r t)").bitcast(F32).rearrange("p (r u) -> p r u", u=2),
                in_=turned.rearrange("p u r -> p r u"),
            )

        def interleave(engine_copy, dst, src, a, b):
            engine_copy(
                out=dst[:, a:b, :].rearrange("p (c i) t -> p c t i", i=4),
                in_=src[:, :, a:b].rearrange("p t (c i) -> p c t i", i=4),
            )

        def interleave_on_gpsimd(dst, src):
            for a in range(0, D, P):
                gps.tensor_scalar(
                    out=dst[:, a : a + P, :], in0=src[:, :, a : a + P].rearrange("p t d -> p d t"),
                    scalar1=1.0, scalar2=0.0, op0=ALU.mult, op1=ALU.add,
                )

        def quantise(name, src, fmt):
            codes = kept(name + "_codes", [P, D], U32)
            scales = kept(name + "_scales", [P, D], U8)
            vec.quantize_mx(out=codes[:].bitcast(fmt), scales=scales[:], in_=src[:].rearrange("p c t -> p (c t)"))
            return codes, scales

        def multiply(out, left, left_fmt, cols, right, right_fmt, start, stop):
            pe.matmul_mx(
                out=out, lhsT=left[0][:, cols].bitcast(left_fmt), lhsT_scale=left[1][:, cols],
                rhs=right[0][:].bitcast(right_fmt), rhs_scale=right[1][:], start=start, stop=stop,
            )

        turned, mask, masked, mm = {}, {}, {}, {}

        def turn_m(k, g):
            turned[k, g] = bank("turn%d" % g, [P, 2, ROWS])
            for i in range(2):
                if k == 0:
                    words = first_m[g][:, i, :].bitcast(F32)
                else:
                    words = m_sb[k][:, i, PASS * g : PASS * (g + 1)].bitcast(F32)
                turn(turned[k, g][:, :, P * i : P * (i + 1)], words)
            if g in CUT_ON_SCALAR[k]:
                cut_on_scalar(k, g)

        def values(k, g):
            return turned[k, g][:].rearrange("p u r -> p (u r)").bitcast(BF16).rearrange("p (u r e) -> p u r e", u=2, e=2)

        def cut_on_scalar(k, g):
            cut = streamed("cut", [P, 2, ROWS, 2], BF16, 4)
            x = values(k, g)
            for u in range(2):
                for e in range(2):
                    t = 2 * u + e
                    act.activation(out=cut[:, u, :, e], in_=x[:, u, :, e], func=ACT.Relu, scale=STEEP, bias=cut_bias[:, g, t : t + 1])
            mask[k, g] = cut

        def compare(k, g, a=0, b=ROWS):
            if g in CUT_ON_SCALAR[k]:
                return
            if a == 0:
                mask[k, g] = streamed("mask", [P, ROWS, PACK], BF16, 4)
            limits = limit_bf[:, g, :].rearrange("p (u e) -> p u e", u=2).unsqueeze(1).to_broadcast([P, b - a, 2, 2])
            vec.tensor_tensor(
                out=mask[k, g][:, a:b, :].rearrange("p r (u e) -> p r u e", u=2),
                in0=values(k, g)[:, :, a:b, :].rearrange("p u r e -> p r u e"), in1=limits, op=ALU.is_gt,
            )

        def apply_mask(k, g, a=0, b=ROWS):
            if a == 0:
                masked[k, g] = streamed("masked", [P, ROWS, PACK], BF16, 4)
            if g in CUT_ON_SCALAR[k]:
                other, op = mask[k, g][:, :, a:b, :].rearrange("p u r e -> p r u e"), ALU.min
            else:
                other, op = mask[k, g][:, a:b, :].rearrange("p r (u e) -> p r u e", u=2), ALU.mult
            vec.tensor_tensor(
                out=masked[k, g][:, a:b, :].rearrange("p r (u e) -> p r u e", u=2),
                in0=values(k, g)[:, :, a:b, :].rearrange("p u r e -> p r u e"), in1=other, op=op,
            )

        def mask_two(k, g):
            compare(k, g)
            compare(k, g + 1)
            apply_mask(k, g)
            apply_mask(k, g + 1)

        def quantise_mm(k, g, a=0, b=ROWS):
            if k not in mm:
                mm[k] = (streamed("mm_codes", [P, PASSES, ROWS], U32, 3), streamed("mm_scales", [P, PASSES, ROWS], U8, 3))
            codes, scales = mm[k]
            vec.quantize_mx(
                out=codes[:, g, a:b].bitcast(E4M3), scales=scales[:, g, a:b],
                in_=masked[k, g][:, a:b, :].rearrange("p r t -> p (r t)"),
            )

        dz2_rows, dz2_sorted, dz2 = {}, {}, {}

        def scale_dz2(q):
            dz2_rows[q] = streamed("dz2_rows", [P, PACK, D], BF16, 2)
            for t in range(PACK):
                vec.tensor_scalar(
                    out=dz2_rows[q][:, t, :], in0=g_sb[q][:, t, :], scalar1=factor[:, q, t : t + 1], scalar2=None, op0=ALU.mult,
                )
            dz2_sorted[q] = streamed("dz2_sorted", [P, D, PACK], BF16, 3)
            if q % 2 == 0:
                interleave(act.copy, dz2_sorted[q], dz2_rows[q], 0, D)
            else:
                interleave_on_gpsimd(dz2_sorted[q], dz2_rows[q])

        def quantise_dz2(q):
            dz2[q] = quantise("dz2_%d" % q, dz2_sorted[q], E5M2)

        dh, dz1 = {}, {}

        def place(k, i):
            return k // 2, 2 * (k % 2) + i

        def multiply_dh(k, i, passes=range(PASSES)):
            if passes[0] == 0:
                dh[k, i] = bank("dh%d" % i, [P, D])
            for g in passes:
                left = (mm[k][0][:, g, :], mm[k][1][:, g, :])
                multiply(dh[k, i][:], left, E4M3, slice(P * i, P * (i + 1)), dz2[g], E5M2, g == 0, g == PASSES - 1)

        def add_g(k, i):
            q, t = place(k, i)
            if t == 0:
                dz1[q] = streamed("dz1", [P, PACK, D], BF16, 2)
            vec.scalar_tensor_tensor(
                out=dz1[q][:, t, :], in0=g_sb[q][:, t, :], scalar=no_edge[:, q, t : t + 1], in1=dh[k, i][:],
                op0=ALU.mult, op1=ALU.add,
            )

        dz1_turned, dz1_f, dz1_fq, out_bank, out_sb = {}, {}, {}, {}, {}

        def turn_dz1(k, i):
            q, t = place(k, i)
            if i == 0:
                dz1_turned[k] = bank("xt", [P, 2, ROWS])
            turn(dz1_turned[k][:, :, P * i : P * (i + 1)], dz1[q][:, t, :].bitcast(F32))

        def straighten_dz1(k, a=0, b=ROWS):
            if a == 0:
                dz1_f[k] = streamed("dz1_f", [P, ROWS, PACK], BF16, 2)
            straighten(dz1_f[k][:, a:b, :], dz1_turned[k][:, :, a:b])

        def quantise_dz1_f(k, a=0, b=ROWS):
            if a == 0:
                dz1_fq[k] = (streamed("dz1_f_codes", [P, ROWS], U32, 4), streamed("dz1_f_scales", [P, ROWS], U8, 4))
            codes, scales = dz1_fq[k]
            vec.quantize_mx(
                out=codes[:, a:b].bitcast(E5M2), scales=scales[:, a:b], in_=dz1_f[k][:, a:b, :].rearrange("p r t -> p (r t)"),
            )

        def multiply_out0(k, i, where):
            out_bank[k, i] = bank(where, [P, D])
            multiply(out_bank[k, i][:], dz1_fq[k], E5M2, slice(P * i, P * (i + 1)), wq, E4M3, True, True)

        def empty_out0(k, i):
            if i == 0:
                out_sb[k] = streamed("out_sb", [P, 2, D], F32, 3)
            act.copy(out=out_sb[k][:, i, :], in_=out_bank[k, i][:])

        def store_out0(k):
            q, t = place(k, 0)
            sync.dma_start(out=o_rows[q][:, t : t + 2, :], in_=out_sb[k][:])

        def finish_out0(k):
            empty_out0(k, 0)
            empty_out0(k, 1)
            store_out0(k)

        dz1_n, dz1_nq, h_n, hq, sums = {}, {}, {}, {}, {}

        def interleave_dz1(q):
            dz1_n[q] = streamed("dz1_n", [P, D, PACK], BF16, 2)
            interleave_on_gpsimd(dz1_n[q], dz1[q])

        def quantise_dz1_n(q):
            dz1_nq[q] = quantise("dz1_n%d" % q, dz1_n[q], E5M2)

        def interleave_h(q):
            h_n[q] = streamed("h_n", [P, D, PACK], BF16, 1)
            interleave_on_gpsimd(h_n[q], h_sb[q])

        def interleave_last_h(half):
            q = PASSES - 1
            if half == 0:
                h_n[q] = kept("h_n_last", [P, D, PACK], BF16)
            interleave(act.copy, h_n[q], h_sb[q], ROWS * half, ROWS * (half + 1))

        def quantise_h(q):
            hq[q] = quantise("h%dq" % q, h_n[q], E4M3)

        def multiply_out1(c, q):
            if q == 0:
                sums[c] = bank("turn%d" % c, [P, D])
            multiply(sums[c][:], hq[q], E4M3, slice(P * c, P * (c + 1)), dz1_nq[q], E5M2, q == 0, q == PASSES - 1)

        w_f = kept("w_f", [P, D, PACK], BF16)

        def turn_w():
            halves = []
            for n, where in enumerate(("xt", "o")):
                b = bank(where, [P, 2, ROWS])
                for i in range(2):
                    turn(b[:, :, P * i : P * (i + 1)], w_sb[:, 2 * n + i, :].bitcast(F32))
                halves.append(b)
            for n in range(2):
                straighten(w_f[:, ROWS * n : ROWS * (n + 1), :], halves[n][:])

        for g in range(PASSES):
            turn_m(0, g)
        compare(0, 0)
        compare(0, 1)
        scale_dz2(0)
        apply_mask(0, 0)
        apply_mask(0, 1)
        turn_m(1, 0)
        turn_m(1, 1)
        scale_dz2(1)
        mask_two(0, 2)
        turn_m(1, 2)
        turn_m(1, 3)
        for g in range(PASSES):
            quantise_mm(0, g)
        load_m(5)
        load_h(2)
        load_h(3)

        scale_dz2(2)
        mask_two(1, 0)
        scale_dz2(3)
        turn_w()
        turn_m(2, 0)
        turn_m(2, 1)
        quantise_dz2(0)
        quantise_dz2(1)
        multiply_dh(0, 0, (0, 1))
        multiply_dh(0, 1, (0, 1))
        mask_two(1, 2)
        quantise_dz2(2)
        quantise_dz2(3)
        turn_m(2, 2)
        turn_m(2, 3)
        multiply_dh(0, 0, (2, 3))
        multiply_dh(0, 1, (2, 3))
        for g in range(PASSES):
            quantise_mm(1, g)
        load_m(6)

        mask_two(2, 0)
        turn_m(3, 0)
        turn_m(3, 1)
        compare(2, 2)
        compare(2, 3)
        add_g(0, 0)
        multiply_dh(1, 0)
        interleave_h(0)
        apply_mask(2, 2)
        apply_mask(2, 3)
        add_g(0, 1)
        multiply_dh(1, 1)
        turn_dz1(0, 0)
        turn_dz1(0, 1)
        straighten_dz1(0)
        turn_m(3, 2)
        turn_m(3, 3)
        quantise_mm(2, 0)
        quantise_mm(2, 1)
        add_g(1, 0)
        quantise_mm(2, 2)
        quantise_mm(2, 3)
        add_g(1, 1)
        load_m(7)

        for k in range(3, LAST):
            if k > 3:
                finish_out0(k - 4)
            multiply_dh(k - 1, 0)
            turn_dz1(k - 2, 0)
            turn_dz1(k - 2, 1)
            straighten_dz1(k - 2)
            mask_two(k, 0)
            if k > 3:
                add_g(k - 1, 0)
            turn_m(k + 1, 0)
            turn_m(k + 1, 1)
            if k == 3:
                interleave_dz1(0)
            elif k == 4:
                interleave_h(1)
                interleave_last_h(0)
            elif k == 5:
                interleave_dz1(1)
                interleave_last_h(1)
            else:
                interleave_h(2)
            multiply_dh(k - 1, 1)
            mask_two(k, 2)
            turn_m(k + 1, 2)
            turn_m(k + 1, 3)
            if k == 3:
                add_g(2, 0)
                quantise_dz1_f(0)
                wq = quantise("w_f", w_f, E4M3)
            multiply_out0(k - 3, 0, "o")
            multiply_out0(k - 3, 1, "dh1")
            quantise_dz1_f(k - 2)
            quantise_mm(k, 0)
            quantise_mm(k, 1)
            if k % 2 == 1:
                add_g(k - 1, 1)
            quantise_mm(k, 2)
            quantise_mm(k, 3)
            if k % 2 == 1:
                quantise_h((k - 3) // 2)
            else:
                quantise_dz1_n((k - 4) // 2)
                add_g(k - 1, 1)

        interleave_dz1(2)
        finish_out0(3)
        multiply_dh(6, 0)
        turn_dz1(5, 0)
        turn_dz1(5, 1)
        straighten_dz1(5)
        multiply_dh(6, 1)
        for g in range(PASSES):
            compare(LAST, g, 0, P)
        add_g(6, 0)
        for g in range(PASSES):
            apply_mask(LAST, g, 0, P)
        multiply_out0(4, 0, "o")
        empty_out0(4, 0)
        multiply_out0(4, 1, "dh1")
        empty_out0(4, 1)
        store_out0(4)
        for g in range(PASSES):
            quantise_mm(LAST, g, 0, P)
        add_g(6, 1)
        multiply_dh(LAST, 0)
        turn_dz1(6, 0)
        turn_dz1(6, 1)
        straighten_dz1(6)
        quantise_dz1_f(5)
        quantise_h(2)
        multiply_out0(5, 0, "o")
        multiply_out0(5, 1, "dh1")
        finish_out0(5)
        for g in range(PASSES):
            compare(LAST, g, P, ROWS)
        add_g(LAST, 0)
        quantise_dz1_f(6)
        turn_dz1(LAST, 0)
        straighten_dz1(LAST, 0, P)
        multiply_out0(6, 0, "o")
        multiply_out0(6, 1, "dh0")
        finish_out0(6)
        for g in range(PASSES):
            apply_mask(LAST, g, P, ROWS)
        multiply_out1(0, 0)
        multiply_out1(0, 1)
        for g in range(PASSES):
            quantise_mm(LAST, g, P, ROWS)
            multiply_dh(LAST, 1, (g,))
        quantise_dz1_f(LAST, 0, P)
        quantise_dz1_n(2)
        multiply_out1(1, 0)
        multiply_out1(1, 1)
        multiply_out0(LAST, 0, "o")
        empty_out0(LAST, 0)
        sync.dma_start(out=o_rows[PASSES - 1][:, 2, :], in_=out_sb[LAST][:, 0, :])
        add_g(LAST, 1)
        turn_dz1(LAST, 1)
        straighten_dz1(LAST, P, ROWS)
        last_n = streamed("dz1_n", [P, D, PACK], BF16, 2)
        dz1_n[PASSES - 1] = last_n
        interleave(vec.tensor_copy, last_n, dz1[PASSES - 1], 0, VECTOR_COLUMNS)
        interleave(act.copy, last_n, dz1[PASSES - 1], VECTOR_COLUMNS, D)
        for c in (2, 3):
            multiply_out1(c, 0)
            multiply_out1(c, 1)
        for c in range(3):
            multiply_out1(c, 2)
        quantise_dz1_f(LAST, P, ROWS)
        quantise_h(PASSES - 1)
        multiply_out0(LAST, 1, "dh1")
        empty_out0(LAST, 1)
        sync.dma_start(out=o_rows[PASSES - 1][:, 3, :], in_=out_sb[LAST][:, 1, :])
        multiply_out1(3, 2)
        quantise_dz1_n(PASSES - 1)
        for c in range(D // P):
            multiply_out1(c, PASSES - 1)
            result = kept("out1_%d" % c, [P, D], F32)
            if c % 2 == 0:
                vec.tensor_copy(out=result[:], in_=sums[c][:])
            else:
                act.copy(out=result[:], in_=sums[c][:])
            sync.dma_start(out=out_1[P * c : P * (c + 1), :], in_=result[:])
